import numpy as np
import ml_dtypes


def mxq(x, axis, fmt="e4m3"):
    dtype, down = {"e4m3": (ml_dtypes.float8_e4m3fn, 7), "e5m2": (ml_dtypes.float8_e5m2, 14)}[fmt]
    v = np.moveaxis(np.asarray(x, np.float32).astype(ml_dtypes.bfloat16).astype(np.float64), axis, -1)
    blocks = v.reshape(v.shape[:-1] + (-1, 32))
    amax = np.abs(blocks).max(-1, keepdims=True)
    byte = np.maximum(np.where(amax > 0, np.frexp(amax)[1] - 1 + 127, 0) - down, 1)
    scale = np.exp2(byte - 127.0)
    codes = (blocks / scale).astype(np.float32).astype(dtype).astype(np.float64)
    return np.moveaxis((codes * scale).reshape(v.shape), -1, axis)


WIDE = False


def mx_kscale(k):
    if not WIDE:
        return np.ones(k)
    levels = np.array([10, -10, 5, -5, 0])
    a = np.random.permutation(np.resize(levels, k // 512 * 4)).reshape(k // 512, 4)
    idx = np.arange(k)
    return np.exp2(a[idx // 512, idx % 128 // 32])


BF16 = ml_dtypes.bfloat16


def bf(x):
    return np.asarray(x, np.float32).astype(BF16)


def f64(x):
    return np.asarray(x).astype(np.float64)


E, B, IN, H, O = 5, 2048, 71, 512, 64
O2 = O + O


def silu(v):
    return v / (1.0 + np.exp(-v))


def softplus(v):
    return np.maximum(v, 0.0) + np.log(1.0 + np.exp(-np.abs(v)))


def setup_inputs():
    s = mx_kscale(H)
    return {"h2": bf(silu(np.random.standard_normal((E, B, H))) * s),
            "w3": bf(np.random.standard_normal((E, H, H)) * 1.6 / np.sqrt(H) / s[:, None]),
            "b3": bf(np.random.standard_normal((E, 1, H)) * 0.2),
            "w4": bf(np.random.standard_normal((E, H, O2)) * 2.5 / np.sqrt(H)),
            "b4": bf(np.random.standard_normal((E, 1, O2)) * 0.2),
            "max_logvar": bf(0.5 + 0.1 * np.random.standard_normal((1, O))),
            "min_logvar": bf(-1.5 + 0.1 * np.random.standard_normal((1, O)))}


def reference(h2, w3, b3, w4, b4, max_logvar, min_logvar):
    h3 = silu((mxq(f64(h2), 2, "e4m3") @ mxq(f64(w3), 1, "e4m3")) + f64(b3))
    o = (mxq(h3, 2, "e4m3") @ mxq(f64(w4), 1, "e4m3")) + f64(b4)
    mean, logvar = o[..., :O], o[..., O:]
    logvar = f64(max_logvar) - softplus(f64(max_logvar) - logvar)
    logvar = f64(min_logvar) + softplus(logvar - f64(min_logvar))
    return mean, logvar

@@ -1,0 +1,313 @@
+import concourse.mybir as mybir
+from concourse.masks import make_identity
+
+F32 = mybir.dt.float32
+BF16 = mybir.dt.bfloat16
+U32 = mybir.dt.uint32
+U8 = mybir.dt.uint8
+FP8X4 = mybir.dt.float8_e4m3fn_x4
+ACT = mybir.ActivationFunctionType
+ALU = mybir.AluOpType
+
+E, B, H, O = 5, 2048, 512, 64
+O2 = 2 * O
+FLOPS = 2 * E * B * H * (H + O2)
+
+P = 128
+PACK = 4
+assert H == P * PACK
+
+ROWS_PER_PARTITION = B // P
+TILES = 4
+CHUNK = TILES * P
+CHUNKS_PER_MEMBER = B // CHUNK
+N_CHUNKS = E * CHUNKS_PER_MEMBER
+H2_BUFS = 8
+
+
+def tile_ensembledynamicsmodel_pa_kernel(
+    tc, h2, w3, b3, w4, b4, max_logvar, min_logvar, out_0, out_1
+):
+    nc = tc.nc
+
+    h2_chunks = h2.rearrange("e (p g r) k -> e g p (r k)", g=CHUNKS_PER_MEMBER, r=TILES)
+    mean_rows = out_0.rearrange("e (p r) o -> e p r o", r=ROWS_PER_PARTITION)
+    logvar_rows = out_1.rearrange("e (p r) o -> e p r o", r=ROWS_PER_PARTITION)
+    w3_rows = w3.rearrange("e (u p i) n -> e p u (i n)", u=2, i=2)
+    w4_rows = w4.rearrange("e (t p) n -> e p t n", p=P)
+
+    with tc.tile_pool(name="const", bufs=1) as const, tc.tile_pool(
+        name="w_raw", bufs=E
+    ) as w_raw, tc.tile_pool(name="w_grouped", bufs=2) as w_grouped, tc.tile_pool(
+        name="w_mx", bufs=E
+    ) as w_mx, tc.tile_pool(name="h2_in", bufs=H2_BUFS) as h2_in, tc.tile_pool(
+        name="stage", bufs=3
+    ) as stage, tc.tile_pool(name="outs", bufs=E) as outs, tc.psum_pool(
+        name="psum_t", bufs=2
+    ) as psum_t, tc.psum_pool(name="psum_1", bufs=4) as psum_1, tc.psum_pool(
+        name="psum_2", bufs=2
+    ) as psum_2, tc.manual_schedule():
+        h2_raw = {}
+        w3_raw = {}
+        w4_raw = {}
+
+        def load_weights(e):
+            w3_in = w_raw.tile([P, 2, 2 * H], BF16)
+            nc.sync.dma_start(out=w3_in[:], in_=w3_rows[e])
+            w4_in = w_raw.tile([P, PACK, O2], BF16)
+            nc.sync.dma_start(out=w4_in[:], in_=w4_rows[e])
+            w3_raw[e] = w3_in
+            w4_raw[e] = w4_in
+
+        def load_chunk(i):
+            h2_rows = h2_in.tile([P, TILES * H], BF16)
+            nc.sync.dma_start(
+                out=h2_rows[:], in_=h2_chunks[i // CHUNKS_PER_MEMBER, i % CHUNKS_PER_MEMBER]
+            )
+            h2_raw[i] = h2_rows
+
+        MAX_AT = E * O2
+        MIN_AT = MAX_AT + O
+        VECTORS = MIN_AT + O
+        vector_rows = const.tile([P, VECTORS], BF16)
+        nc.vector.memset(vector_rows[:], 0.0)
+        nc.scalar.dma_start(out=vector_rows[0:1, MAX_AT:MIN_AT], in_=max_logvar)
+        nc.scalar.dma_start(out=vector_rows[0:1, MIN_AT:VECTORS], in_=min_logvar)
+        nc.scalar.dma_start(out=vector_rows[0:1, 0:MAX_AT], in_=b4.rearrange("e o n -> o (e n)"))
+        b3_rows = const.tile([P, P], BF16)
+        nc.vector.memset(b3_rows[:], 0.0)
+        nc.scalar.dma_start(
+            out=b3_rows[0 : E * PACK, :], in_=b3.rearrange("e o (t p) -> (e o t) p", p=P)
+        )
+
+        load_weights(0)
+        for i in range(H2_BUFS):
+            load_chunk(i)
+            if 1 <= i < E:
+                load_weights(i)
+
+        identity = const.tile([P, P], F32)
+        make_identity(nc, identity[:])
+        ones = const.tile([P, P], BF16)
+        nc.vector.memset(ones[:], 1.0)
+
+        spread = const.tile([P, VECTORS], F32)
+        for lo in range(0, VECTORS, CHUNK):
+            width = min(CHUNK, VECTORS - lo)
+            spread_ps = psum_t.tile([P, CHUNK], F32, tag="xt")
+            nc.tensor.matmul(
+                out=spread_ps[:, 0:width],
+                lhsT=ones[:],
+                rhs=vector_rows[:, lo : lo + width],
+                start=True,
+                stop=True,
+            )
+            nc.vector.tensor_copy(out=spread[:, lo : lo + width], in_=spread_ps[:, 0:width])
+        max_spread = spread[:, MAX_AT:MIN_AT]
+        min_spread = spread[:, MIN_AT:VECTORS]
+        o_shift = spread[:, 0:MAX_AT].rearrange("p (e n) -> p e n", e=E)
+        nc.vector.tensor_tensor(
+            out=o_shift[:, :, O:O2],
+            in0=o_shift[:, :, O:O2],
+            in1=max_spread.unsqueeze(1).to_broadcast([P, E, O]),
+            op=ALU.subtract,
+        )
+        gap = const.tile([P, O], F32)
+        nc.vector.tensor_tensor(out=gap[:], in0=min_spread, in1=max_spread, op=ALU.subtract)
+        exp_gap = const.tile([P, O], F32)
+        nc.scalar.activation(out=exp_gap[:], in_=gap[:], func=ACT.Exp)
+        table_warmer = const.tile([P, 1], F32)
+        nc.scalar.activation(out=table_warmer[:], in_=gap[:, 0:1], func=ACT.Silu)
+
+        b3_rows_f32 = const.tile([P, P], F32)
+        nc.vector.tensor_copy(out=b3_rows_f32[:], in_=b3_rows[:])
+        b3_ps = psum_t.tile([P, P], F32, tag="xt")
+        nc.tensor.transpose(b3_ps[:], b3_rows_f32[:], identity[:])
+        b3_cols = const.tile([P, P], F32)
+        nc.vector.tensor_copy(out=b3_cols[:], in_=b3_ps[:])
+
+        w3_mx = {}
+        w4_mx = {}
+
+        def regroup(dst, src):
+            nc.vector.tensor_copy(
+                out=dst.rearrange("p (c i) t -> p c t i", i=4),
+                in_=src.rearrange("p t (c i) -> p c t i", i=4),
+            )
+
+        def prepare_weights(e):
+            w3_grouped = w_grouped.tile([P, H, PACK], BF16, align_bytes=64)
+            regroup(w3_grouped[:], w3_raw[e][:].rearrange("p u (i n) -> p (u i) n", i=2))
+            w4_grouped = w_grouped.tile([P, O2, PACK], BF16, align_bytes=64)
+            regroup(w4_grouped[:], w4_raw[e][:])
+            w3_codes = w_mx.tile([P, H], U32, align_bytes=64)
+            w3_scales = w_mx.tile([P, H], U8, align_bytes=64)
+            nc.vector.quantize_mx(
+                out=w3_codes[:].bitcast(FP8X4),
+                scales=w3_scales[:],
+                in_=w3_grouped[:].rearrange("p c t -> p (c t)"),
+            )
+            w4_codes = w_mx.tile([P, O2], U32, align_bytes=64)
+            w4_scales = w_mx.tile([P, O2], U8, align_bytes=64)
+            nc.vector.quantize_mx(
+                out=w4_codes[:].bitcast(FP8X4),
+                scales=w4_scales[:],
+                in_=w4_grouped[:].rearrange("p c t -> p (c t)"),
+            )
+            w3_mx[e] = (w3_codes, w3_scales)
+            w4_mx[e] = (w4_codes, w4_scales)
+
+        h2_t = {}
+        h2_grouped = {}
+        h2_mx = {}
+        h3_ps = {}
+        h3_planes = {}
+        h3_grouped = {}
+        h3_mx = {}
+        o_ps = {}
+        o_sb = {}
+
+        def transpose_h2(i):
+            words = h2_raw[i][:].bitcast(F32)
+            banks = []
+            for b in range(2):
+                xt = psum_t.tile([P, 2, 2, P], F32, tag="xt")
+                for j in range(2):
+                    for u in range(2):
+                        first = (2 * b + j) * (H // 2) + u * P
+                        nc.tensor.transpose(xt[:, j, u, :], words[:, first : first + P], identity[:])
+                banks.append(xt)
+            h2_t[i] = banks
+
+        def copy_h2(i):
+            grouped = stage.tile([P, CHUNK * PACK], BF16, align_bytes=64, tag="h2_grouped")
+            grouped_words = grouped[:].bitcast(F32)
+            for b in range(2):
+                nc.scalar.copy(
+                    out=grouped_words[:, b * CHUNK : (b + 1) * CHUNK].rearrange(
+                        "p (j c u) -> p j c u", j=2, u=2
+                    ),
+                    in_=h2_t[i][b][:].rearrange("p j u c -> p j c u"),
+                )
+            h2_grouped[i] = grouped
+
+        def quantise(grouped, tag):
+            codes = stage.tile([P, CHUNK], U32, align_bytes=64, tag=tag + "_codes")
+            scales = stage.tile([P, CHUNK], U8, align_bytes=64, tag=tag + "_scales")
+            nc.vector.quantize_mx(out=codes[:].bitcast(FP8X4), scales=scales[:], in_=grouped)
+            return codes, scales
+
+        def first_product(i):
+            w3_codes, w3_scales = w3_mx[i // CHUNKS_PER_MEMBER]
+            h2_codes, h2_scales = h2_mx[i]
+            banks = []
+            for t in range(PACK):
+                features = slice(t * P, (t + 1) * P)
+                acc = psum_1.tile([P, CHUNK], F32)
+                nc.tensor.matmul_mx(
+                    out=acc[:],
+                    lhsT=w3_codes[:, features].bitcast(FP8X4),
+                    lhsT_scale=w3_scales[:, features],
+                    rhs=h2_codes[:].bitcast(FP8X4),
+                    rhs_scale=h2_scales[:],
+                    start=True,
+                    stop=True,
+                )
+                banks.append(acc)
+            h3_ps[i] = banks
+
+        def silu_h3(i):
+            e = i // CHUNKS_PER_MEMBER
+            planes = stage.tile([P, PACK, CHUNK], BF16, tag="h3_planes")
+            for t in range(PACK):
+                nc.scalar.activation(
+                    out=planes[:, t, :],
+                    in_=h3_ps[i][t][:],
+                    func=ACT.Silu,
+                    bias=b3_cols[:, e * PACK + t : e * PACK + t + 1],
+                )
+            h3_planes[i] = planes
+
+        def regroup_h3(i):
+            grouped = stage.tile([P, CHUNK, PACK], BF16, align_bytes=64, tag="h3_grouped")
+            regroup(grouped[:], h3_planes[i][:])
+            h3_grouped[i] = grouped
+
+        def second_product(i):
+            w4_codes, w4_scales = w4_mx[i // CHUNKS_PER_MEMBER]
+            h3_codes, h3_scales = h3_mx[i]
+            acc = psum_2.tile([P, TILES, O2], F32)
+            for r in range(TILES):
+                rows = slice(r * P, (r + 1) * P)
+                nc.tensor.matmul_mx(
+                    out=acc[:, r, :],
+                    lhsT=h3_codes[:, rows].bitcast(FP8X4),
+                    lhsT_scale=h3_scales[:, rows],
+                    rhs=w4_codes[:].bitcast(FP8X4),
+                    rhs_scale=w4_scales[:],
+                    start=True,
+                    stop=True,
+                )
+            o_ps[i] = acc
+
+        def shift_o(i):
+            e, g = i // CHUNKS_PER_MEMBER, i % CHUNKS_PER_MEMBER
+            if g == 0:
+                o_member = outs.tile([P, ROWS_PER_PARTITION, O2], F32)
+                o_sb[e] = o_member
+            nc.vector.tensor_tensor(
+                out=o_sb[e][:, g * TILES : (g + 1) * TILES, :],
+                in0=o_ps[i][:],
+                in1=o_shift[:, e, :].unsqueeze(1).to_broadcast([P, TILES, O2]),
+                op=ALU.add,
+            )
+            if g == CHUNKS_PER_MEMBER - 1:
+                nc.sync.dma_start(out=mean_rows[e], in_=o_sb[e][:, :, 0:O])
+
+        def live(i):
+            return 0 <= i < N_CHUNKS
+
+        for s in range(-3, N_CHUNKS + 1):
+            if live(s + 2):
+                copy_h2(s + 2)
+            if live(s + 1):
+                silu_h3(s + 1)
+            if live(s):
+                regroup_h3(s)
+            if live(s + 2):
+                h2_mx[s + 2] = quantise(h2_grouped[s + 2][:], "h2")
+            if live(s):
+                h3_mx[s] = quantise(h3_grouped[s][:].rearrange("p c t -> p (c t)"), "h3")
+            if live(s - 1):
+                shift_o(s - 1)
+            if s + 3 < E:
+                prepare_weights(s + 3)
+            if live(s + 3):
+                transpose_h2(s + 3)
+                if live(s + 3 + H2_BUFS):
+                    load_chunk(s + 3 + H2_BUFS)
+            if live(s):
+                second_product(s)
+            if live(s + 2):
+                first_product(s + 2)
+
+        logvar = {}
+        for e in range(E):
+            bounded = outs.tile([P, ROWS_PER_PARTITION, O], F32)
+            nc.scalar.activation(out=bounded[:], in_=o_sb[e][:, :, O:O2], func=ACT.Sigmoid)
+            nc.vector.tensor_tensor(
+                out=bounded[:],
+                in0=bounded[:],
+                in1=exp_gap[:].unsqueeze(1).to_broadcast([P, ROWS_PER_PARTITION, O]),
+                op=ALU.add,
+            )
+            logvar[e] = bounded
+        for e in range(E):
+            nc.scalar.activation(out=logvar[e][:], in_=logvar[e][:], func=ACT.Ln)
+            nc.vector.tensor_tensor(
+                out=logvar[e][:],
+                in0=logvar[e][:],
+                in1=max_spread.unsqueeze(1).to_broadcast([P, ROWS_PER_PARTITION, O]),
+                op=ALU.add,
+            )
+            nc.sync.dma_start(out=logvar_rows[e], in_=logvar[e][:])

@@ -23,6 +23,9 @@ CHUNK = TILES * P
 CHUNKS_PER_MEMBER = B // CHUNK
 N_CHUNKS = E * CHUNKS_PER_MEMBER
 H2_BUFS = 8
+WEIGHTS_LEAD = 6
+BOUND_TILES = ROWS_PER_PARTITION // 2
+SPREAD_STEP = -1
 
 
 def tile_ensembledynamicsmodel_pa_kernel(
@@ -47,6 +50,9 @@ def tile_ensembledynamicsmodel_pa_kernel(
     ) as psum_t, tc.psum_pool(name="psum_1", bufs=4) as psum_1, tc.psum_pool(
         name="psum_2", bufs=2
     ) as psum_2, tc.manual_schedule():
+        def live(i):
+            return 0 <= i < N_CHUNKS
+
         h2_raw = {}
         w3_raw = {}
         w4_raw = {}
@@ -66,66 +72,72 @@ def tile_ensembledynamicsmodel_pa_kernel(
             )
             h2_raw[i] = h2_rows
 
+        b3_rows = const.tile([P, P], BF16)
+        nc.vector.memset(b3_rows[:], 0.0)
         MAX_AT = E * O2
         MIN_AT = MAX_AT + O
         VECTORS = MIN_AT + O
         vector_rows = const.tile([P, VECTORS], BF16)
         nc.vector.memset(vector_rows[:], 0.0)
-        nc.scalar.dma_start(out=vector_rows[0:1, MAX_AT:MIN_AT], in_=max_logvar)
-        nc.scalar.dma_start(out=vector_rows[0:1, MIN_AT:VECTORS], in_=min_logvar)
-        nc.scalar.dma_start(out=vector_rows[0:1, 0:MAX_AT], in_=b4.rearrange("e o n -> o (e n)"))
-        b3_rows = const.tile([P, P], BF16)
-        nc.vector.memset(b3_rows[:], 0.0)
-        nc.scalar.dma_start(
+
+        load_chunk(0)
+        load_weights(0)
+        nc.sync.dma_start(
             out=b3_rows[0 : E * PACK, :], in_=b3.rearrange("e o (t p) -> (e o t) p", p=P)
         )
-
-        load_weights(0)
-        for i in range(H2_BUFS):
+        load_chunk(1)
+        nc.sync.dma_start(out=vector_rows[0:1, 0:MAX_AT], in_=b4.rearrange("e o n -> o (e n)"))
+        nc.sync.dma_start(out=vector_rows[0:1, MAX_AT:MIN_AT], in_=max_logvar)
+        nc.sync.dma_start(out=vector_rows[0:1, MIN_AT:VECTORS], in_=min_logvar)
+        for i in range(2, H2_BUFS):
+            if i - 1 < E:
+                load_weights(i - 1)
             load_chunk(i)
-            if 1 <= i < E:
-                load_weights(i)
+
+        ones = const.tile([P, P], BF16)
+        nc.vector.memset(ones[:], 1.0)
+        table_warmer = const.tile([P, 1], F32)
+        nc.scalar.activation(out=table_warmer[:], in_=ones[:, 0:1], func=ACT.Silu)
 
         identity = const.tile([P, P], F32)
         make_identity(nc, identity[:])
-        ones = const.tile([P, P], BF16)
-        nc.vector.memset(ones[:], 1.0)
+
+        b3_cols = const.tile([P, P], F32)
+
+        def transpose_b3():
+            b3_rows_f32 = const.tile([P, P], F32)
+            nc.vector.tensor_copy(out=b3_rows_f32[:], in_=b3_rows[:])
+            b3_ps = psum_2.tile([P, P], F32, tag="o_ps")
+            nc.tensor.transpose(b3_ps[:], b3_rows_f32[:], identity[:])
+            nc.vector.tensor_copy(out=b3_cols[:], in_=b3_ps[:])
 
         spread = const.tile([P, VECTORS], F32)
-        for lo in range(0, VECTORS, CHUNK):
-            width = min(CHUNK, VECTORS - lo)
-            spread_ps = psum_t.tile([P, CHUNK], F32, tag="xt")
-            nc.tensor.matmul(
-                out=spread_ps[:, 0:width],
-                lhsT=ones[:],
-                rhs=vector_rows[:, lo : lo + width],
-                start=True,
-                stop=True,
-            )
-            nc.vector.tensor_copy(out=spread[:, lo : lo + width], in_=spread_ps[:, 0:width])
         max_spread = spread[:, MAX_AT:MIN_AT]
         min_spread = spread[:, MIN_AT:VECTORS]
         o_shift = spread[:, 0:MAX_AT].rearrange("p (e n) -> p e n", e=E)
-        nc.vector.tensor_tensor(
-            out=o_shift[:, :, O:O2],
-            in0=o_shift[:, :, O:O2],
-            in1=max_spread.unsqueeze(1).to_broadcast([P, E, O]),
-            op=ALU.subtract,
-        )
         gap = const.tile([P, O], F32)
-        nc.vector.tensor_tensor(out=gap[:], in0=min_spread, in1=max_spread, op=ALU.subtract)
-        exp_gap = const.tile([P, O], F32)
-        nc.scalar.activation(out=exp_gap[:], in_=gap[:], func=ACT.Exp)
-        table_warmer = const.tile([P, 1], F32)
-        nc.scalar.activation(out=table_warmer[:], in_=gap[:, 0:1], func=ACT.Silu)
 
-        b3_rows_f32 = const.tile([P, P], F32)
-        nc.vector.tensor_copy(out=b3_rows_f32[:], in_=b3_rows[:])
-        b3_ps = psum_t.tile([P, P], F32, tag="xt")
-        nc.tensor.transpose(b3_ps[:], b3_rows_f32[:], identity[:])
-        b3_cols = const.tile([P, P], F32)
-        nc.vector.tensor_copy(out=b3_cols[:], in_=b3_ps[:])
+        def spread_vectors():
+            for lo in range(0, VECTORS, CHUNK):
+                width = min(CHUNK, VECTORS - lo)
+                spread_ps = psum_2.tile([P, CHUNK], F32, tag="o_ps")
+                nc.tensor.matmul(
+                    out=spread_ps[:, 0:width],
+                    lhsT=ones[:],
+                    rhs=vector_rows[:, lo : lo + width],
+                    start=True,
+                    stop=True,
+                )
+                nc.vector.tensor_copy(out=spread[:, lo : lo + width], in_=spread_ps[:, 0:width])
+            nc.vector.tensor_tensor(
+                out=o_shift[:, :, O:O2],
+                in0=o_shift[:, :, O:O2],
+                in1=max_spread.unsqueeze(1).to_broadcast([P, E, O]),
+                op=ALU.subtract,
+            )
+            nc.vector.tensor_tensor(out=gap[:], in0=min_spread, in1=max_spread, op=ALU.subtract)
 
+        w_regrouped = {}
         w3_mx = {}
         w4_mx = {}
 
@@ -135,11 +147,15 @@ def tile_ensembledynamicsmodel_pa_kernel(
                 in_=src.rearrange("p t (c i) -> p c t i", i=4),
             )
 
-        def prepare_weights(e):
+        def regroup_weights(e):
             w3_grouped = w_grouped.tile([P, H, PACK], BF16, align_bytes=64)
             regroup(w3_grouped[:], w3_raw[e][:].rearrange("p u (i n) -> p (u i) n", i=2))
             w4_grouped = w_grouped.tile([P, O2, PACK], BF16, align_bytes=64)
             regroup(w4_grouped[:], w4_raw[e][:])
+            w_regrouped[e] = (w3_grouped, w4_grouped)
+
+        def quantise_weights(e):
+            w3_grouped, w4_grouped = w_regrouped[e]
             w3_codes = w_mx.tile([P, H], U32, align_bytes=64)
             w3_scales = w_mx.tile([P, H], U8, align_bytes=64)
             nc.vector.quantize_mx(
@@ -171,13 +187,15 @@ def tile_ensembledynamicsmodel_pa_kernel(
             words = h2_raw[i][:].bitcast(F32)
             banks = []
             for b in range(2):
-                xt = psum_t.tile([P, 2, 2, P], F32, tag="xt")
+                xt = psum_t.tile([P, 2, 2, P], F32)
                 for j in range(2):
                     for u in range(2):
                         first = (2 * b + j) * (H // 2) + u * P
                         nc.tensor.transpose(xt[:, j, u, :], words[:, first : first + P], identity[:])
                 banks.append(xt)
             h2_t[i] = banks
+            if live(i + H2_BUFS):
+                load_chunk(i + H2_BUFS)
 
         def copy_h2(i):
             grouped = stage.tile([P, CHUNK * PACK], BF16, align_bytes=64, tag="h2_grouped")
@@ -236,7 +254,7 @@ def tile_ensembledynamicsmodel_pa_kernel(
         def second_product(i):
             w4_codes, w4_scales = w4_mx[i // CHUNKS_PER_MEMBER]
             h3_codes, h3_scales = h3_mx[i]
-            acc = psum_2.tile([P, TILES, O2], F32)
+            acc = psum_2.tile([P, TILES, O2], F32, tag="o_ps")
             for r in range(TILES):
                 rows = slice(r * P, (r + 1) * P)
                 nc.tensor.matmul_mx(
@@ -264,10 +282,14 @@ def tile_ensembledynamicsmodel_pa_kernel(
             if g == CHUNKS_PER_MEMBER - 1:
                 nc.sync.dma_start(out=mean_rows[e], in_=o_sb[e][:, :, 0:O])
 
-        def live(i):
-            return 0 <= i < N_CHUNKS
+        def first_chunk_of_member(i):
+            return live(i) and i % CHUNKS_PER_MEMBER == 0
 
-        for s in range(-3, N_CHUNKS + 1):
+        transpose_h2(0)
+        regroup_weights(0)
+        quantise_weights(0)
+        transpose_b3()
+        for s in range(-2, N_CHUNKS + 1):
             if live(s + 2):
                 copy_h2(s + 2)
             if live(s + 1):
@@ -280,34 +302,50 @@ def tile_ensembledynamicsmodel_pa_kernel(
                 h3_mx[s] = quantise(h3_grouped[s][:].rearrange("p c t -> p (c t)"), "h3")
             if live(s - 1):
                 shift_o(s - 1)
-            if s + 3 < E:
-                prepare_weights(s + 3)
+            if first_chunk_of_member(s + WEIGHTS_LEAD):
+                regroup_weights((s + WEIGHTS_LEAD) // CHUNKS_PER_MEMBER)
+            if first_chunk_of_member(s + WEIGHTS_LEAD - 1):
+                quantise_weights((s + WEIGHTS_LEAD - 1) // CHUNKS_PER_MEMBER)
+            if s == SPREAD_STEP:
+                spread_vectors()
             if live(s + 3):
                 transpose_h2(s + 3)
-                if live(s + 3 + H2_BUFS):
-                    load_chunk(s + 3 + H2_BUFS)
             if live(s):
                 second_product(s)
             if live(s + 2):
                 first_product(s + 2)
 
+        gap_up = const.tile([P, O], F32)
+        nc.scalar.activation(out=gap_up[:], in_=gap[:], func=ACT.Sigmoid)
+        gap_down = const.tile([P, O], F32)
+        nc.scalar.activation(out=gap_down[:], in_=gap[:], func=ACT.Sigmoid, scale=-1.0)
+        exp_gap = const.tile([P, O], F32)
+        nc.vector.reciprocal(out=exp_gap[:], in_=gap_down[:])
+        nc.vector.tensor_tensor(out=exp_gap[:], in0=exp_gap[:], in1=gap_up[:], op=ALU.mult)
+
+        pieces = [(e, lo) for e in range(E) for lo in range(0, ROWS_PER_PARTITION, BOUND_TILES)]
         logvar = {}
-        for e in range(E):
-            bounded = outs.tile([P, ROWS_PER_PARTITION, O], F32)
-            nc.scalar.activation(out=bounded[:], in_=o_sb[e][:, :, O:O2], func=ACT.Sigmoid)
+        for e, lo in pieces:
+            if lo == 0:
+                bounded = outs.tile([P, ROWS_PER_PARTITION, O], F32)
+                logvar[e] = bounded
+            piece = logvar[e][:, lo : lo + BOUND_TILES, :]
+            nc.scalar.activation(
+                out=piece, in_=o_sb[e][:, lo : lo + BOUND_TILES, O:O2], func=ACT.Sigmoid
+            )
             nc.vector.tensor_tensor(
-                out=bounded[:],
-                in0=bounded[:],
-                in1=exp_gap[:].unsqueeze(1).to_broadcast([P, ROWS_PER_PARTITION, O]),
+                out=piece,
+                in0=piece,
+                in1=exp_gap[:].unsqueeze(1).to_broadcast([P, BOUND_TILES, O]),
                 op=ALU.add,
             )
-            logvar[e] = bounded
-        for e in range(E):
-            nc.scalar.activation(out=logvar[e][:], in_=logvar[e][:], func=ACT.Ln)
+        for e, lo in pieces:
+            piece = logvar[e][:, lo : lo + BOUND_TILES, :]
+            nc.scalar.activation(out=piece, in_=piece, func=ACT.Ln)
             nc.vector.tensor_tensor(
-                out=logvar[e][:],
-                in0=logvar[e][:],
-                in1=max_spread.unsqueeze(1).to_broadcast([P, ROWS_PER_PARTITION, O]),
+                out=piece,
+                in0=piece,
+                in1=max_spread.unsqueeze(1).to_broadcast([P, BOUND_TILES, O]),
                 op=ALU.add,
             )
-            nc.sync.dma_start(out=logvar_rows[e], in_=logvar[e][:])
+            nc.sync.dma_start(out=logvar_rows[e][:, lo : lo + BOUND_TILES, :], in_=piece)

@@ -49,7 +49,7 @@ def tile_ensembledynamicsmodel_pa_kernel(
         name="psum_t", bufs=2
     ) as psum_t, tc.psum_pool(name="psum_1", bufs=4) as psum_1, tc.psum_pool(
         name="psum_2", bufs=2
-    ) as psum_2, tc.manual_schedule():
+    ) as psum_2:
         def live(i):
             return 0 <= i < N_CHUNKS
 

@@ -24,7 +24,11 @@ CHUNKS_PER_MEMBER = B // CHUNK
 N_CHUNKS = E * CHUNKS_PER_MEMBER
 H2_BUFS = 8
 WEIGHTS_LEAD = 6
-BOUND_TILES = ROWS_PER_PARTITION // 2
+PAIR = 2
+N_PAIRS = N_CHUNKS // PAIR
+PAIR_ROWS = PAIR * TILES
+SQUARINGS = 3
+VECTOR_SHARE = 2
 SPREAD_STEP = -1
 
 
@@ -45,11 +49,13 @@ def tile_ensembledynamicsmodel_pa_kernel(
         name="w_mx", bufs=E
     ) as w_mx, tc.tile_pool(name="h2_in", bufs=H2_BUFS) as h2_in, tc.tile_pool(
         name="stage", bufs=3
-    ) as stage, tc.tile_pool(name="outs", bufs=E) as outs, tc.psum_pool(
-        name="psum_t", bufs=2
-    ) as psum_t, tc.psum_pool(name="psum_1", bufs=4) as psum_1, tc.psum_pool(
-        name="psum_2", bufs=2
-    ) as psum_2:
+    ) as stage, tc.tile_pool(name="tanhs", bufs=N_PAIRS) as tanhs, tc.tile_pool(
+        name="outs", bufs=E
+    ) as outs, tc.psum_pool(name="psum_t", bufs=2) as psum_t, tc.psum_pool(
+        name="psum_1", bufs=4
+    ) as psum_1, tc.psum_pool(name="psum_mean", bufs=1) as psum_mean, tc.psum_pool(
+        name="psum_raw", bufs=1
+    ) as psum_raw:
         def live(i):
             return 0 <= i < N_CHUNKS
 
@@ -74,11 +80,12 @@ def tile_ensembledynamicsmodel_pa_kernel(
 
         b3_rows = const.tile([P, P], BF16)
         nc.vector.memset(b3_rows[:], 0.0)
-        MAX_AT = E * O2
-        MIN_AT = MAX_AT + O
-        VECTORS = MIN_AT + O
-        vector_rows = const.tile([P, VECTORS], BF16)
-        nc.vector.memset(vector_rows[:], 0.0)
+        MAX_ROW, MIN_ROW = E, E + 1
+        bound_rows = const.tile([P, O2], BF16)
+        nc.vector.memset(bound_rows[:], 0.0)
+        nc.gpsimd.dma_start(out=bound_rows[0:E, :], in_=b4.rearrange("e o n -> (e o) n"))
+        nc.gpsimd.dma_start(out=bound_rows[MAX_ROW : MAX_ROW + 1, O:O2], in_=max_logvar)
+        nc.gpsimd.dma_start(out=bound_rows[MIN_ROW : MIN_ROW + 1, O:O2], in_=min_logvar)
 
         load_chunk(0)
         load_weights(0)
@@ -86,58 +93,98 @@ def tile_ensembledynamicsmodel_pa_kernel(
             out=b3_rows[0 : E * PACK, :], in_=b3.rearrange("e o (t p) -> (e o t) p", p=P)
         )
         load_chunk(1)
-        nc.sync.dma_start(out=vector_rows[0:1, 0:MAX_AT], in_=b4.rearrange("e o n -> o (e n)"))
-        nc.sync.dma_start(out=vector_rows[0:1, MAX_AT:MIN_AT], in_=max_logvar)
-        nc.sync.dma_start(out=vector_rows[0:1, MIN_AT:VECTORS], in_=min_logvar)
         for i in range(2, H2_BUFS):
             if i - 1 < E:
                 load_weights(i - 1)
             load_chunk(i)
 
-        ones = const.tile([P, P], BF16)
-        nc.vector.memset(ones[:], 1.0)
+        warm_input = const.tile([P, 1], F32)
+        nc.vector.memset(warm_input[:], 1.0)
         table_warmer = const.tile([P, 1], F32)
-        nc.scalar.activation(out=table_warmer[:], in_=ones[:, 0:1], func=ACT.Silu)
+        nc.scalar.activation(out=table_warmer[:], in_=warm_input[:], func=ACT.Silu)
 
         identity = const.tile([P, P], F32)
         make_identity(nc, identity[:])
 
+        row_picker = const.tile([P, P], BF16)
+        make_identity(nc, row_picker[:])
+
+        def columns_of(cols, rows_f32):
+            cols_ps = psum_mean.tile([P, P], F32, tag="mean_ps")
+            nc.tensor.transpose(cols_ps[:], rows_f32[:], identity[:])
+            nc.vector.tensor_copy(out=cols[:], in_=cols_ps[:])
+
         b3_cols = const.tile([P, P], F32)
 
         def transpose_b3():
-            b3_rows_f32 = const.tile([P, P], F32)
-            nc.vector.tensor_copy(out=b3_rows_f32[:], in_=b3_rows[:])
-            b3_ps = psum_2.tile([P, P], F32, tag="o_ps")
-            nc.tensor.transpose(b3_ps[:], b3_rows_f32[:], identity[:])
-            nc.vector.tensor_copy(out=b3_cols[:], in_=b3_ps[:])
+            b3_f32 = const.tile([P, P], F32)
+            nc.vector.tensor_copy(out=b3_f32[:], in_=b3_rows[:])
+            columns_of(b3_cols, b3_f32)
 
-        spread = const.tile([P, VECTORS], F32)
-        max_spread = spread[:, MAX_AT:MIN_AT]
-        min_spread = spread[:, MIN_AT:VECTORS]
-        o_shift = spread[:, 0:MAX_AT].rearrange("p (e n) -> p e n", e=E)
-        gap = const.tile([P, O], F32)
+        tanh_bias = const.tile([P, E], F32)
+        ln_bias = const.tile([P, 1], F32)
+
+        def prepare_bounds():
+            raw_rows = const.tile([P, 2, O], F32)
+            nc.vector.tensor_copy(
+                out=raw_rows[:], in_=bound_rows[:, O:O2].unsqueeze(1).to_broadcast([P, 2, O])
+            )
+            bound_cols = const.tile([P, P], F32)
+            columns_of(bound_cols, raw_rows[:].rearrange("p h o -> p (h o)"))
+            max_col = bound_cols[:, MAX_ROW : MAX_ROW + 1]
+            nc.vector.tensor_scalar(
+                out=tanh_bias[:],
+                in0=bound_cols[:, 0:E],
+                scalar1=max_col,
+                scalar2=0.5,
+                op0=ALU.subtract,
+                op1=ALU.mult,
+            )
+            gap = const.tile([P, 1], F32)
+            nc.vector.tensor_tensor(
+                out=gap[:], in0=bound_cols[:, MIN_ROW : MIN_ROW + 1], in1=max_col, op=ALU.subtract
+            )
+            gap_tanh = const.tile([P, 1], F32)
+            nc.scalar.activation(
+                out=gap_tanh[:], in_=gap[:], func=ACT.Tanh, scale=0.5 / 2**SQUARINGS
+            )
+            below = const.tile([P, 1], F32)
+            nc.vector.tensor_scalar(
+                out=below[:], in0=gap_tanh[:], scalar1=-1.0, scalar2=1.0, op0=ALU.mult, op1=ALU.add
+            )
+            nc.vector.reciprocal(out=below[:], in_=below[:])
+            power = const.tile([P, 1], F32)
+            nc.vector.scalar_tensor_tensor(
+                out=power[:], in0=gap_tanh[:], scalar=1.0, in1=below[:], op0=ALU.add, op1=ALU.mult
+            )
+            for i in range(SQUARINGS):
+                nc.vector.tensor_tensor(out=power[:], in0=power[:], in1=power[:], op=ALU.mult)
+            nc.vector.tensor_scalar_add(ln_bias[:], power[:], 0.5)
+
+        mean_shift = const.tile([P, E, O], F32)
+        max_spread = const.tile([P, O], F32)
 
         def spread_vectors():
-            for lo in range(0, VECTORS, CHUNK):
-                width = min(CHUNK, VECTORS - lo)
-                spread_ps = psum_2.tile([P, CHUNK], F32, tag="o_ps")
+            spread_ps = psum_mean.tile([P, E + 1, O], F32, tag="mean_ps")
+            for j in range(E + 1):
                 nc.tensor.matmul(
-                    out=spread_ps[:, 0:width],
-                    lhsT=ones[:],
-                    rhs=vector_rows[:, lo : lo + width],
+                    out=spread_ps[:, j, :],
+                    lhsT=row_picker[:, j : j + 1].to_broadcast([P, P]),
+                    rhs=bound_rows[:, O:O2] if j == MAX_ROW else bound_rows[:, 0:O],
                     start=True,
                     stop=True,
                 )
-                nc.vector.tensor_copy(out=spread[:, lo : lo + width], in_=spread_ps[:, 0:width])
-            nc.vector.tensor_tensor(
-                out=o_shift[:, :, O:O2],
-                in0=o_shift[:, :, O:O2],
-                in1=max_spread.unsqueeze(1).to_broadcast([P, E, O]),
-                op=ALU.subtract,
-            )
-            nc.vector.tensor_tensor(out=gap[:], in0=min_spread, in1=max_spread, op=ALU.subtract)
+            nc.vector.tensor_copy(out=mean_shift[:], in_=spread_ps[:, 0:E, :])
+            nc.vector.tensor_copy(out=max_spread[:], in_=spread_ps[:, MAX_ROW, :])
 
-        w_regrouped = {}
+        MEAN_COLS = slice(0, O)
+        RAW_COLS = slice(2 * O, 3 * O)
+        RAW_HALF = (slice(2 * O, 4 * O), slice(O, 3 * O))
+        w4_grouped = const.tile([P, E, 4 * O, PACK], BF16, align_bytes=64)
+        for zeros in (slice(O, 2 * O), slice(3 * O, 4 * O)):
+            nc.vector.memset(w4_grouped[:, :, zeros, :], 0.0)
+
+        w3_regrouped = {}
         w3_mx = {}
         w4_mx = {}
 
@@ -150,25 +197,24 @@ def tile_ensembledynamicsmodel_pa_kernel(
         def regroup_weights(e):
             w3_grouped = w_grouped.tile([P, H, PACK], BF16, align_bytes=64)
             regroup(w3_grouped[:], w3_raw[e][:].rearrange("p u (i n) -> p (u i) n", i=2))
-            w4_grouped = w_grouped.tile([P, O2, PACK], BF16, align_bytes=64)
-            regroup(w4_grouped[:], w4_raw[e][:])
-            w_regrouped[e] = (w3_grouped, w4_grouped)
+            w3_regrouped[e] = w3_grouped
+            regroup(w4_grouped[:, e, MEAN_COLS, :], w4_raw[e][:, :, 0:O])
+            regroup(w4_grouped[:, e, RAW_COLS, :], w4_raw[e][:, :, O:O2])
 
         def quantise_weights(e):
-            w3_grouped, w4_grouped = w_regrouped[e]
             w3_codes = w_mx.tile([P, H], U32, align_bytes=64)
             w3_scales = w_mx.tile([P, H], U8, align_bytes=64)
             nc.vector.quantize_mx(
                 out=w3_codes[:].bitcast(FP8X4),
                 scales=w3_scales[:],
-                in_=w3_grouped[:].rearrange("p c t -> p (c t)"),
+                in_=w3_regrouped[e][:].rearrange("p c t -> p (c t)"),
             )
-            w4_codes = w_mx.tile([P, O2], U32, align_bytes=64)
-            w4_scales = w_mx.tile([P, O2], U8, align_bytes=64)
+            w4_codes = w_mx.tile([P, 4 * O], U32, align_bytes=64)
+            w4_scales = w_mx.tile([P, 4 * O], U8, align_bytes=64)
             nc.vector.quantize_mx(
                 out=w4_codes[:].bitcast(FP8X4),
                 scales=w4_scales[:],
-                in_=w4_grouped[:].rearrange("p c t -> p (c t)"),
+                in_=w4_grouped[:, e].rearrange("p c t -> p (c t)"),
             )
             w3_mx[e] = (w3_codes, w3_scales)
             w4_mx[e] = (w4_codes, w4_scales)
@@ -180,8 +226,11 @@ def tile_ensembledynamicsmodel_pa_kernel(
         h3_planes = {}
         h3_grouped = {}
         h3_mx = {}
-        o_ps = {}
-        o_sb = {}
+        mean_ps = {}
+        raw_ps = {}
+        mean_sb = {}
+        tanh_sb = {}
+        logvar_sb = {}
 
         def transpose_h2(i):
             words = h2_raw[i][:].bitcast(F32)
@@ -201,7 +250,8 @@ def tile_ensembledynamicsmodel_pa_kernel(
             grouped = stage.tile([P, CHUNK * PACK], BF16, align_bytes=64, tag="h2_grouped")
             grouped_words = grouped[:].bitcast(F32)
             for b in range(2):
-                nc.scalar.copy(
+                on_vector = b == 1 and i % VECTOR_SHARE == VECTOR_SHARE - 1
+                (nc.vector.tensor_copy if on_vector else nc.scalar.copy)(
                     out=grouped_words[:, b * CHUNK : (b + 1) * CHUNK].rearrange(
                         "p (j c u) -> p j c u", j=2, u=2
                     ),
@@ -254,33 +304,54 @@ def tile_ensembledynamicsmodel_pa_kernel(
         def second_product(i):
             w4_codes, w4_scales = w4_mx[i // CHUNKS_PER_MEMBER]
             h3_codes, h3_scales = h3_mx[i]
-            acc = psum_2.tile([P, TILES, O2], F32, tag="o_ps")
+            pair, half = i // PAIR, i % PAIR
+            if half == 0:
+                mean_acc = psum_mean.tile([P, PAIR_ROWS, O], F32, tag="mean_ps")
+                raw_acc = psum_raw.tile([P, CHUNK], F32)
+                mean_ps[pair] = mean_acc
+                raw_ps[pair] = raw_acc
+            nc.tensor.matmul_mx(
+                out=raw_ps[pair][:],
+                lhsT=w4_codes[:, RAW_HALF[half]].bitcast(FP8X4),
+                lhsT_scale=w4_scales[:, RAW_HALF[half]],
+                rhs=h3_codes[:].bitcast(FP8X4),
+                rhs_scale=h3_scales[:],
+                start=(half == 0),
+                stop=(half == PAIR - 1),
+            )
             for r in range(TILES):
                 rows = slice(r * P, (r + 1) * P)
                 nc.tensor.matmul_mx(
-                    out=acc[:, r, :],
+                    out=mean_ps[pair][:, half * TILES + r, :],
                     lhsT=h3_codes[:, rows].bitcast(FP8X4),
                     lhsT_scale=h3_scales[:, rows],
-                    rhs=w4_codes[:].bitcast(FP8X4),
-                    rhs_scale=w4_scales[:],
+                    rhs=w4_codes[:, MEAN_COLS].bitcast(FP8X4),
+                    rhs_scale=w4_scales[:, MEAN_COLS],
                     start=True,
                     stop=True,
                 )
-            o_ps[i] = acc
 
-        def shift_o(i):
-            e, g = i // CHUNKS_PER_MEMBER, i % CHUNKS_PER_MEMBER
-            if g == 0:
-                o_member = outs.tile([P, ROWS_PER_PARTITION, O2], F32)
-                o_sb[e] = o_member
+        def tanh_raw(pair):
+            e = pair * PAIR // CHUNKS_PER_MEMBER
+            th = tanhs.tile([P, CHUNK], F32)
+            nc.scalar.activation(
+                out=th[:], in_=raw_ps[pair][:], func=ACT.Tanh, bias=tanh_bias[:, e : e + 1], scale=0.5
+            )
+            tanh_sb[pair] = th
+
+        def shift_mean(pair):
+            e, h = divmod(pair, CHUNKS_PER_MEMBER // PAIR)
+            if h == 0:
+                mean_member = outs.tile([P, ROWS_PER_PARTITION, O], F32)
+                mean_sb[e] = mean_member
             nc.vector.tensor_tensor(
-                out=o_sb[e][:, g * TILES : (g + 1) * TILES, :],
-                in0=o_ps[i][:],
-                in1=o_shift[:, e, :].unsqueeze(1).to_broadcast([P, TILES, O2]),
+                out=mean_sb[e][:, h * PAIR_ROWS : (h + 1) * PAIR_ROWS, :],
+                in0=mean_ps[pair][:],
+                in1=mean_shift[:, e, :].unsqueeze(1).to_broadcast([P, PAIR_ROWS, O]),
                 op=ALU.add,
             )
-            if g == CHUNKS_PER_MEMBER - 1:
-                nc.sync.dma_start(out=mean_rows[e], in_=o_sb[e][:, :, 0:O])
+            if (h + 1) * PAIR == CHUNKS_PER_MEMBER:
+                nc.sync.dma_start(out=mean_rows[e], in_=mean_sb[e][:])
 
         def first_chunk_of_member(i):
             return live(i) and i % CHUNKS_PER_MEMBER == 0
@@ -294,20 +365,23 @@ def tile_ensembledynamicsmodel_pa_kernel(
                 copy_h2(s + 2)
             if live(s + 1):
                 silu_h3(s + 1)
+            if live(s - 1) and s % PAIR == 0:
+                tanh_raw((s - 1) // PAIR)
             if live(s):
                 regroup_h3(s)
             if live(s + 2):
                 h2_mx[s + 2] = quantise(h2_grouped[s + 2][:], "h2")
             if live(s):
                 h3_mx[s] = quantise(h3_grouped[s][:].rearrange("p c t -> p (c t)"), "h3")
-            if live(s - 1):
-                shift_o(s - 1)
+            if live(s - 1) and s % PAIR == 0:
+                shift_mean((s - 1) // PAIR)
             if first_chunk_of_member(s + WEIGHTS_LEAD):
                 regroup_weights((s + WEIGHTS_LEAD) // CHUNKS_PER_MEMBER)
             if first_chunk_of_member(s + WEIGHTS_LEAD - 1):
                 quantise_weights((s + WEIGHTS_LEAD - 1) // CHUNKS_PER_MEMBER)
             if s == SPREAD_STEP:
                 spread_vectors()
+                prepare_bounds()
             if live(s + 3):
                 transpose_h2(s + 3)
             if live(s):
@@ -315,37 +389,26 @@ def tile_ensembledynamicsmodel_pa_kernel(
             if live(s + 2):
                 first_product(s + 2)
 
-        gap_up = const.tile([P, O], F32)
-        nc.scalar.activation(out=gap_up[:], in_=gap[:], func=ACT.Sigmoid)
-        gap_down = const.tile([P, O], F32)
-        nc.scalar.activation(out=gap_down[:], in_=gap[:], func=ACT.Sigmoid, scale=-1.0)
-        exp_gap = const.tile([P, O], F32)
-        nc.vector.reciprocal(out=exp_gap[:], in_=gap_down[:])
-        nc.vector.tensor_tensor(out=exp_gap[:], in0=exp_gap[:], in1=gap_up[:], op=ALU.mult)
-
-        pieces = [(e, lo) for e in range(E) for lo in range(0, ROWS_PER_PARTITION, BOUND_TILES)]
-        logvar = {}
-        for e, lo in pieces:
-            if lo == 0:
-                bounded = outs.tile([P, ROWS_PER_PARTITION, O], F32)
-                logvar[e] = bounded
-            piece = logvar[e][:, lo : lo + BOUND_TILES, :]
+        for pair in range(N_PAIRS):
             nc.scalar.activation(
-                out=piece, in_=o_sb[e][:, lo : lo + BOUND_TILES, O:O2], func=ACT.Sigmoid
+                out=tanh_sb[pair][:], in_=tanh_sb[pair][:], func=ACT.Ln, bias=ln_bias[:], scale=0.5
             )
+            acc = psum_1.tile([P, TILES, PAIR, O], F32)
+            for r in range(TILES):
+                nc.tensor.transpose(
+                    acc[:, r, :, :].rearrange("p a o -> p (a o)"),
+                    tanh_sb[pair][:, r * P : (r + 1) * P],
+                    identity[:],
+                )
+            e, h = divmod(pair, CHUNKS_PER_MEMBER // PAIR)
+            if h == 0:
+                logvar_member = outs.tile([P, ROWS_PER_PARTITION, O], F32)
+                logvar_sb[e] = logvar_member
+            rows = slice(h * PAIR_ROWS, (h + 1) * PAIR_ROWS)
             nc.vector.tensor_tensor(
-                out=piece,
-                in0=piece,
-                in1=exp_gap[:].unsqueeze(1).to_broadcast([P, BOUND_TILES, O]),
+                out=logvar_sb[e][:, rows, :].rearrange("p (a r) o -> p r a o", a=PAIR),
+                in0=acc[:],
+                in1=max_spread[:].unsqueeze(1).unsqueeze(1).to_broadcast([P, TILES, PAIR, O]),
                 op=ALU.add,
             )
-        for e, lo in pieces:
-            piece = logvar[e][:, lo : lo + BOUND_TILES, :]
-            nc.scalar.activation(out=piece, in_=piece, func=ACT.Ln)
-            nc.vector.tensor_tensor(
-                out=piece,
-                in0=piece,
-                in1=max_spread.unsqueeze(1).to_broadcast([P, BOUND_TILES, O]),
-                op=ALU.add,
-            )
-            nc.sync.dma_start(out=logvar_rows[e][:, lo : lo + BOUND_TILES, :], in_=piece)
+            nc.sync.dma_start(out=logvar_rows[e][:, rows, :], in_=logvar_sb[e][:, rows, :])

@@ -23,12 +23,13 @@ CHUNK = TILES * P
 CHUNKS_PER_MEMBER = B // CHUNK
 N_CHUNKS = E * CHUNKS_PER_MEMBER
 H2_BUFS = 8
-WEIGHTS_LEAD = 6
+WEIGHTS_LEAD = 5
 PAIR = 2
 N_PAIRS = N_CHUNKS // PAIR
 PAIR_ROWS = PAIR * TILES
 SQUARINGS = 3
-VECTOR_SHARE = 2
+HEAD_PARTS = 2
+VECTOR_COPIES = (3,)
 SPREAD_STEP = -1
 
 
@@ -40,7 +41,7 @@ def tile_ensembledynamicsmodel_pa_kernel(
     h2_chunks = h2.rearrange("e (p g r) k -> e g p (r k)", g=CHUNKS_PER_MEMBER, r=TILES)
     mean_rows = out_0.rearrange("e (p r) o -> e p r o", r=ROWS_PER_PARTITION)
     logvar_rows = out_1.rearrange("e (p r) o -> e p r o", r=ROWS_PER_PARTITION)
-    w3_rows = w3.rearrange("e (u p i) n -> e p u (i n)", u=2, i=2)
+    w3_rows = w3.rearrange("e (u p i) n -> e p u i n", u=2, i=2)
     w4_rows = w4.rearrange("e (t p) n -> e p t n", p=P)
 
     with tc.tile_pool(name="const", bufs=1) as const, tc.tile_pool(
@@ -63,23 +64,42 @@ def tile_ensembledynamicsmodel_pa_kernel(
         w3_raw = {}
         w4_raw = {}
 
-        def load_weights(e):
-            w3_in = w_raw.tile([P, 2, 2 * H], BF16)
-            nc.sync.dma_start(out=w3_in[:], in_=w3_rows[e])
+        def load_w3(e):
+            parts = HEAD_PARTS if e == 0 else 1
+            w3_raw[e] = []
+            for n in range(0, H, H // parts):
+                w3_in = w_raw.tile([P, 2, 2, H // parts], BF16, tag="w3_in_%d" % parts)
+                for u in range(2):
+                    nc.sync.dma_start(
+                        out=w3_in[:, u], in_=w3_rows[e][:, u, :, n : n + H // parts]
+                    )
+                w3_raw[e].append(w3_in)
+
+        def load_w4(e):
             w4_in = w_raw.tile([P, PACK, O2], BF16)
             nc.sync.dma_start(out=w4_in[:], in_=w4_rows[e])
-            w3_raw[e] = w3_in
             w4_raw[e] = w4_in
 
-        def load_chunk(i):
+        def load_chunk(i, parts=1):
             h2_rows = h2_in.tile([P, TILES * H], BF16)
-            nc.sync.dma_start(
-                out=h2_rows[:], in_=h2_chunks[i // CHUNKS_PER_MEMBER, i % CHUNKS_PER_MEMBER]
-            )
+            for at in range(0, TILES * H, TILES * H // parts):
+                part = slice(at, at + TILES * H // parts)
+                nc.sync.dma_start(
+                    out=h2_rows[:, part],
+                    in_=h2_chunks[i // CHUNKS_PER_MEMBER, i % CHUNKS_PER_MEMBER][:, part],
+                )
             h2_raw[i] = h2_rows
+
+        identity = const.tile([P, P], F32)
+        make_identity(nc, identity[:])
+        row_picker = const.tile([P, P], BF16)
+        make_identity(nc, row_picker[:])
 
         b3_rows = const.tile([P, P], BF16)
         nc.vector.memset(b3_rows[:], 0.0)
+        nc.scalar.dma_start(
+            out=b3_rows[0 : E * PACK, :], in_=b3.rearrange("e o (t p) -> (e o t) p", p=P)
+        )
         MAX_ROW, MIN_ROW = E, E + 1
         bound_rows = const.tile([P, O2], BF16)
         nc.vector.memset(bound_rows[:], 0.0)
@@ -87,27 +107,20 @@ def tile_ensembledynamicsmodel_pa_kernel(
         nc.gpsimd.dma_start(out=bound_rows[MAX_ROW : MAX_ROW + 1, O:O2], in_=max_logvar)
         nc.gpsimd.dma_start(out=bound_rows[MIN_ROW : MIN_ROW + 1, O:O2], in_=min_logvar)
 
-        load_chunk(0)
-        load_weights(0)
-        nc.sync.dma_start(
-            out=b3_rows[0 : E * PACK, :], in_=b3.rearrange("e o (t p) -> (e o t) p", p=P)
-        )
+        load_chunk(0, parts=HEAD_PARTS)
+        load_w3(0)
         load_chunk(1)
+        load_w4(0)
         for i in range(2, H2_BUFS):
             if i - 1 < E:
-                load_weights(i - 1)
+                load_w3(i - 1)
+                load_w4(i - 1)
             load_chunk(i)
 
         warm_input = const.tile([P, 1], F32)
         nc.vector.memset(warm_input[:], 1.0)
         table_warmer = const.tile([P, 1], F32)
         nc.scalar.activation(out=table_warmer[:], in_=warm_input[:], func=ACT.Silu)
-
-        identity = const.tile([P, P], F32)
-        make_identity(nc, identity[:])
-
-        row_picker = const.tile([P, P], BF16)
-        make_identity(nc, row_picker[:])
 
         def columns_of(cols, rows_f32):
             cols_ps = psum_mean.tile([P, P], F32, tag="mean_ps")
@@ -124,15 +137,19 @@ def tile_ensembledynamicsmodel_pa_kernel(
         tanh_bias = const.tile([P, E], F32)
         ln_bias = const.tile([P, 1], F32)
 
-        def prepare_bounds():
+        bound_cols = const.tile([P, P], F32)
+        gap = const.tile([P, 1], F32)
+        gap_tanh = const.tile([P, 1], F32)
+        max_col = bound_cols[:, MAX_ROW : MAX_ROW + 1]
+        min_col = bound_cols[:, MIN_ROW : MIN_ROW + 1]
+
+        def prepare_tanh_bias():
             raw_rows = const.tile([P, 2, O], F32)
             nc.vector.tensor_copy(
                 out=raw_rows[:], in_=bound_rows[:, O:O2].unsqueeze(1).to_broadcast([P, 2, O])
             )
-            bound_cols = const.tile([P, P], F32)
             columns_of(bound_cols, raw_rows[:].rearrange("p h o -> p (h o)"))
-            max_col = bound_cols[:, MAX_ROW : MAX_ROW + 1]
-            nc.vector.tensor_scalar(
+            nc.gpsimd.tensor_scalar(
                 out=tanh_bias[:],
                 in0=bound_cols[:, 0:E],
                 scalar1=max_col,
@@ -140,26 +157,24 @@ def tile_ensembledynamicsmodel_pa_kernel(
                 op0=ALU.subtract,
                 op1=ALU.mult,
             )
-            gap = const.tile([P, 1], F32)
-            nc.vector.tensor_tensor(
-                out=gap[:], in0=bound_cols[:, MIN_ROW : MIN_ROW + 1], in1=max_col, op=ALU.subtract
-            )
-            gap_tanh = const.tile([P, 1], F32)
+            nc.gpsimd.tensor_tensor(out=gap[:], in0=min_col, in1=max_col, op=ALU.subtract)
+
+        def prepare_ln_bias():
             nc.scalar.activation(
                 out=gap_tanh[:], in_=gap[:], func=ACT.Tanh, scale=0.5 / 2**SQUARINGS
             )
             below = const.tile([P, 1], F32)
-            nc.vector.tensor_scalar(
+            nc.gpsimd.tensor_scalar(
                 out=below[:], in0=gap_tanh[:], scalar1=-1.0, scalar2=1.0, op0=ALU.mult, op1=ALU.add
             )
-            nc.vector.reciprocal(out=below[:], in_=below[:])
+            above = const.tile([P, 1], F32)
+            nc.vector.reciprocal(out=above[:], in_=below[:])
             power = const.tile([P, 1], F32)
-            nc.vector.scalar_tensor_tensor(
-                out=power[:], in0=gap_tanh[:], scalar=1.0, in1=below[:], op0=ALU.add, op1=ALU.mult
-            )
+            nc.gpsimd.tensor_scalar_add(power[:], gap_tanh[:], 1.0)
+            nc.gpsimd.tensor_tensor(out=power[:], in0=power[:], in1=above[:], op=ALU.mult)
             for i in range(SQUARINGS):
-                nc.vector.tensor_tensor(out=power[:], in0=power[:], in1=power[:], op=ALU.mult)
-            nc.vector.tensor_scalar_add(ln_bias[:], power[:], 0.5)
+                nc.gpsimd.tensor_tensor(out=power[:], in0=power[:], in1=power[:], op=ALU.mult)
+            nc.gpsimd.tensor_scalar_add(ln_bias[:], power[:], 0.5)
 
         mean_shift = const.tile([P, E, O], F32)
         max_spread = const.tile([P, O], F32)
@@ -178,7 +193,6 @@ def tile_ensembledynamicsmodel_pa_kernel(
             nc.vector.tensor_copy(out=max_spread[:], in_=spread_ps[:, MAX_ROW, :])
 
         MEAN_COLS = slice(0, O)
-        RAW_COLS = slice(2 * O, 3 * O)
         RAW_HALF = (slice(2 * O, 4 * O), slice(O, 3 * O))
         w4_grouped = const.tile([P, E, 4 * O, PACK], BF16, align_bytes=64)
         for zeros in (slice(O, 2 * O), slice(3 * O, 4 * O)):
@@ -194,21 +208,38 @@ def tile_ensembledynamicsmodel_pa_kernel(
                 in_=src.rearrange("p t (c i) -> p c t i", i=4),
             )
 
-        def regroup_weights(e):
-            w3_grouped = w_grouped.tile([P, H, PACK], BF16, align_bytes=64)
-            regroup(w3_grouped[:], w3_raw[e][:].rearrange("p u (i n) -> p (u i) n", i=2))
-            w3_regrouped[e] = w3_grouped
-            regroup(w4_grouped[:, e, MEAN_COLS, :], w4_raw[e][:, :, 0:O])
-            regroup(w4_grouped[:, e, RAW_COLS, :], w4_raw[e][:, :, O:O2])
+        W3_PARTS = [slice(n, n + H // HEAD_PARTS) for n in range(0, H, H // HEAD_PARTS)]
 
-        def quantise_weights(e):
+        def new_w3(e):
+            w3_grouped = w_grouped.tile([P, H, PACK], BF16, align_bytes=64)
+            w3_regrouped[e] = w3_grouped
             w3_codes = w_mx.tile([P, H], U32, align_bytes=64)
             w3_scales = w_mx.tile([P, H], U8, align_bytes=64)
-            nc.vector.quantize_mx(
-                out=w3_codes[:].bitcast(FP8X4),
-                scales=w3_scales[:],
-                in_=w3_regrouped[e][:].rearrange("p c t -> p (c t)"),
+            w3_mx[e] = (w3_codes, w3_scales)
+
+        def regroup_w3(e, part):
+            raw = w3_raw[e]
+            source = raw[part][:] if len(raw) > 1 else raw[0][:, :, :, W3_PARTS[part]]
+            regroup(
+                w3_regrouped[e][:, W3_PARTS[part], :],
+                source.rearrange("p u i n -> p (u i) n"),
             )
+
+        def quantise_w3(e, cols=slice(0, H)):
+            w3_codes, w3_scales = w3_mx[e]
+            nc.vector.quantize_mx(
+                out=w3_codes[:, cols].bitcast(FP8X4),
+                scales=w3_scales[:, cols],
+                in_=w3_regrouped[e][:, cols, :].rearrange("p c t -> p (c t)"),
+            )
+
+        def regroup_w4(e):
+            nc.vector.tensor_copy(
+                out=w4_grouped[:, e].rearrange("p (h c) t -> p h c t", h=2)[:, :, 0:O, :],
+                in_=w4_raw[e][:].rearrange("p t (h c) -> p h c t", h=2),
+            )
+
+        def quantise_w4(e):
             w4_codes = w_mx.tile([P, 4 * O], U32, align_bytes=64)
             w4_scales = w_mx.tile([P, 4 * O], U8, align_bytes=64)
             nc.vector.quantize_mx(
@@ -216,7 +247,6 @@ def tile_ensembledynamicsmodel_pa_kernel(
                 scales=w4_scales[:],
                 in_=w4_grouped[:, e].rearrange("p c t -> p (c t)"),
             )
-            w3_mx[e] = (w3_codes, w3_scales)
             w4_mx[e] = (w4_codes, w4_scales)
 
         h2_t = {}
@@ -250,7 +280,7 @@ def tile_ensembledynamicsmodel_pa_kernel(
             grouped = stage.tile([P, CHUNK * PACK], BF16, align_bytes=64, tag="h2_grouped")
             grouped_words = grouped[:].bitcast(F32)
             for b in range(2):
-                on_vector = b == 1 and i % VECTOR_SHARE == VECTOR_SHARE - 1
+                on_vector = i == 1 or b == 1 and (i == 0 or i % CHUNKS_PER_MEMBER in VECTOR_COPIES)
                 (nc.vector.tensor_copy if on_vector else nc.scalar.copy)(
                     out=grouped_words[:, b * CHUNK : (b + 1) * CHUNK].rearrange(
                         "p (j c u) -> p j c u", j=2, u=2
@@ -356,59 +386,90 @@ def tile_ensembledynamicsmodel_pa_kernel(
         def first_chunk_of_member(i):
             return live(i) and i % CHUNKS_PER_MEMBER == 0
 
-        transpose_h2(0)
-        regroup_weights(0)
-        quantise_weights(0)
-        transpose_b3()
-        for s in range(-2, N_CHUNKS + 1):
-            if live(s + 2):
-                copy_h2(s + 2)
-            if live(s + 1):
-                silu_h3(s + 1)
-            if live(s - 1) and s % PAIR == 0:
-                tanh_raw((s - 1) // PAIR)
-            if live(s):
-                regroup_h3(s)
-            if live(s + 2):
-                h2_mx[s + 2] = quantise(h2_grouped[s + 2][:], "h2")
-            if live(s):
-                h3_mx[s] = quantise(h3_grouped[s][:].rearrange("p c t -> p (c t)"), "h3")
-            if live(s - 1) and s % PAIR == 0:
-                shift_mean((s - 1) // PAIR)
-            if first_chunk_of_member(s + WEIGHTS_LEAD):
-                regroup_weights((s + WEIGHTS_LEAD) // CHUNKS_PER_MEMBER)
-            if first_chunk_of_member(s + WEIGHTS_LEAD - 1):
-                quantise_weights((s + WEIGHTS_LEAD - 1) // CHUNKS_PER_MEMBER)
-            if s == SPREAD_STEP:
-                spread_vectors()
-                prepare_bounds()
-            if live(s + 3):
-                transpose_h2(s + 3)
-            if live(s):
-                second_product(s)
-            if live(s + 2):
-                first_product(s + 2)
+        with tc.manual_schedule():
+            def quantise_h2(i):
+                h2_mx[i] = quantise(h2_grouped[i][:], "h2")
 
-        for pair in range(N_PAIRS):
-            nc.scalar.activation(
-                out=tanh_sb[pair][:], in_=tanh_sb[pair][:], func=ACT.Ln, bias=ln_bias[:], scale=0.5
-            )
-            acc = psum_1.tile([P, TILES, PAIR, O], F32)
-            for r in range(TILES):
-                nc.tensor.transpose(
-                    acc[:, r, :, :].rearrange("p a o -> p (a o)"),
-                    tanh_sb[pair][:, r * P : (r + 1) * P],
-                    identity[:],
+            transpose_h2(0)
+            copy_h2(0)
+            new_w3(0)
+            regroup_w3(0, 0)
+            quantise_w3(0, W3_PARTS[0])
+            transpose_b3()
+            quantise_h2(0)
+            regroup_w3(0, 1)
+            quantise_w3(0, W3_PARTS[1])
+            first_product(0)
+            transpose_h2(1)
+            copy_h2(1)
+            quantise_h2(1)
+            silu_h3(0)
+            transpose_h2(2)
+            first_product(1)
+            regroup_w4(0)
+            quantise_w4(0)
+            for s in range(N_CHUNKS + 1):
+                if live(s + 2):
+                    copy_h2(s + 2)
+                if live(s - 1) and s % PAIR == 0:
+                    tanh_raw((s - 1) // PAIR)
+                if live(s + 1):
+                    silu_h3(s + 1)
+                if live(s):
+                    regroup_h3(s)
+                if live(s + 2):
+                    quantise_h2(s + 2)
+                if live(s):
+                    h3_mx[s] = quantise(h3_grouped[s][:].rearrange("p c t -> p (c t)"), "h3")
+                if live(s - 1) and s % PAIR == 0:
+                    shift_mean((s - 1) // PAIR)
+                if s == 0:
+                    spread_vectors()
+                    prepare_tanh_bias()
+                if s == 3:
+                    prepare_ln_bias()
+                e, stage_of_weights = divmod(s + WEIGHTS_LEAD, CHUNKS_PER_MEMBER)
+                if 0 < e < E:
+                    if stage_of_weights == 0:
+                        new_w3(e)
+                        regroup_w3(e, 0)
+                    elif stage_of_weights == 1:
+                        if e == 1:
+                            new_w3(e)
+                            regroup_w3(e, 0)
+                        regroup_w3(e, 1)
+                    elif stage_of_weights == 2:
+                        quantise_w3(e)
+                    else:
+                        regroup_w4(e)
+                        quantise_w4(e)
+                if live(s + 3):
+                    transpose_h2(s + 3)
+                if live(s):
+                    second_product(s)
+                if live(s + 2):
+                    first_product(s + 2)
+
+            for pair in range(N_PAIRS):
+                nc.scalar.activation(
+                    out=tanh_sb[pair][:], in_=tanh_sb[pair][:], func=ACT.Ln, bias=ln_bias[:], scale=0.5
                 )
-            e, h = divmod(pair, CHUNKS_PER_MEMBER // PAIR)
-            if h == 0:
-                logvar_member = outs.tile([P, ROWS_PER_PARTITION, O], F32)
-                logvar_sb[e] = logvar_member
-            rows = slice(h * PAIR_ROWS, (h + 1) * PAIR_ROWS)
-            nc.vector.tensor_tensor(
-                out=logvar_sb[e][:, rows, :].rearrange("p (a r) o -> p r a o", a=PAIR),
-                in0=acc[:],
-                in1=max_spread[:].unsqueeze(1).unsqueeze(1).to_broadcast([P, TILES, PAIR, O]),
-                op=ALU.add,
-            )
-            nc.sync.dma_start(out=logvar_rows[e][:, rows, :], in_=logvar_sb[e][:, rows, :])
+                acc = psum_1.tile([P, TILES, PAIR, O], F32)
+                for r in range(TILES):
+                    nc.tensor.transpose(
+                        acc[:, r, :, :].rearrange("p a o -> p (a o)"),
+                        tanh_sb[pair][:, r * P : (r + 1) * P],
+                        identity[:],
+                    )
+                e, h = divmod(pair, CHUNKS_PER_MEMBER // PAIR)
+                if h == 0:
+                    logvar_member = outs.tile([P, ROWS_PER_PARTITION, O], F32)
+                    logvar_sb[e] = logvar_member
+                rows = slice(h * PAIR_ROWS, (h + 1) * PAIR_ROWS)
+                nc.vector.tensor_tensor(
+                    out=logvar_sb[e][:, rows, :].rearrange("p (a r) o -> p r a o", a=PAIR),
+                    in0=acc[:],
+                    in1=max_spread[:].unsqueeze(1).unsqueeze(1).to_broadcast([P, TILES, PAIR, O]),
+                    op=ALU.add,
+                )
+                nc.sync.dma_start(out=logvar_rows[e][:, rows, :], in_=logvar_sb[e][:, rows, :])

@@ -29,7 +29,11 @@ N_PAIRS = N_CHUNKS // PAIR
 PAIR_ROWS = PAIR * TILES
 SQUARINGS = 3
 HEAD_PARTS = 2
-VECTOR_COPIES = (3,)
+VECTOR_COPIES = lambda i: i%4==1
+LOOK = 2
+LAG = 1
+SINGLES = 2
+WSTEP = (4, 4, 3, 2)
 SPREAD_STEP = -1
 
 
@@ -41,17 +45,19 @@ def tile_ensembledynamicsmodel_pa_kernel(
     h2_chunks = h2.rearrange("e (p g r) k -> e g p (r k)", g=CHUNKS_PER_MEMBER, r=TILES)
     mean_rows = out_0.rearrange("e (p r) o -> e p r o", r=ROWS_PER_PARTITION)
     logvar_rows = out_1.rearrange("e (p r) o -> e p r o", r=ROWS_PER_PARTITION)
-    w3_rows = w3.rearrange("e (u p i) n -> e p u i n", u=2, i=2)
+    w3_rows = w3.rearrange("e (u p i) n -> e p u (i n)", u=2, i=2)
     w4_rows = w4.rearrange("e (t p) n -> e p t n", p=P)
 
     with tc.tile_pool(name="const", bufs=1) as const, tc.tile_pool(
         name="w_raw", bufs=E
     ) as w_raw, tc.tile_pool(name="w_grouped", bufs=2) as w_grouped, tc.tile_pool(
-        name="w_mx", bufs=E
+        name="w_mx", bufs=3
     ) as w_mx, tc.tile_pool(name="h2_in", bufs=H2_BUFS) as h2_in, tc.tile_pool(
-        name="stage", bufs=3
-    ) as stage, tc.tile_pool(name="tanhs", bufs=N_PAIRS) as tanhs, tc.tile_pool(
-        name="outs", bufs=E
+        name="stage", bufs=LOOK + 1
+    ) as stage, tc.tile_pool(name="h3_in", bufs=3) as h3_in, tc.tile_pool(
+        name="h3_stage", bufs=2
+    ) as h3_stage, tc.tile_pool(name="logs", bufs=5) as logs, tc.tile_pool(name="tanhs", bufs=N_PAIRS) as tanhs, tc.tile_pool(
+        name="outs", bufs=2
     ) as outs, tc.psum_pool(name="psum_t", bufs=2) as psum_t, tc.psum_pool(
         name="psum_1", bufs=4
     ) as psum_1, tc.psum_pool(name="psum_mean", bufs=1) as psum_mean, tc.psum_pool(
@@ -65,15 +71,9 @@ def tile_ensembledynamicsmodel_pa_kernel(
         w4_raw = {}
 
         def load_w3(e):
-            parts = HEAD_PARTS if e == 0 else 1
-            w3_raw[e] = []
-            for n in range(0, H, H // parts):
-                w3_in = w_raw.tile([P, 2, 2, H // parts], BF16, tag="w3_in_%d" % parts)
-                for u in range(2):
-                    nc.sync.dma_start(
-                        out=w3_in[:, u], in_=w3_rows[e][:, u, :, n : n + H // parts]
-                    )
-                w3_raw[e].append(w3_in)
+            w3_in = w_raw.tile([P, 2, 2 * H], BF16)
+            nc.sync.dma_start(out=w3_in[:], in_=w3_rows[e])
+            w3_raw[e] = w3_in
 
         def load_w4(e):
             w4_in = w_raw.tile([P, PACK, O2], BF16)
@@ -103,12 +103,12 @@ def tile_ensembledynamicsmodel_pa_kernel(
         MAX_ROW, MIN_ROW = E, E + 1
         bound_rows = const.tile([P, O2], BF16)
         nc.vector.memset(bound_rows[:], 0.0)
-        nc.gpsimd.dma_start(out=bound_rows[0:E, :], in_=b4.rearrange("e o n -> (e o) n"))
-        nc.gpsimd.dma_start(out=bound_rows[MAX_ROW : MAX_ROW + 1, O:O2], in_=max_logvar)
-        nc.gpsimd.dma_start(out=bound_rows[MIN_ROW : MIN_ROW + 1, O:O2], in_=min_logvar)
 
-        load_chunk(0, parts=HEAD_PARTS)
         load_w3(0)
+        load_chunk(0, parts=HEAD_PARTS)
+        nc.sync.dma_start(out=bound_rows[0:E, :], in_=b4.rearrange("e o n -> (e o) n"))
+        nc.sync.dma_start(out=bound_rows[MAX_ROW : MAX_ROW + 1, O:O2], in_=max_logvar)
+        nc.sync.dma_start(out=bound_rows[MIN_ROW : MIN_ROW + 1, O:O2], in_=min_logvar)
         load_chunk(1)
         load_w4(0)
         for i in range(2, H2_BUFS):
@@ -122,75 +122,73 @@ def tile_ensembledynamicsmodel_pa_kernel(
         table_warmer = const.tile([P, 1], F32)
         nc.scalar.activation(out=table_warmer[:], in_=warm_input[:], func=ACT.Silu)
 
-        def columns_of(cols, rows_f32):
-            cols_ps = psum_mean.tile([P, P], F32, tag="mean_ps")
-            nc.tensor.transpose(cols_ps[:], rows_f32[:], identity[:])
-            nc.vector.tensor_copy(out=cols[:], in_=cols_ps[:])
-
+        b3_f32 = const.tile([P, P], F32)
         b3_cols = const.tile([P, P], F32)
-
-        def transpose_b3():
-            b3_f32 = const.tile([P, P], F32)
-            nc.vector.tensor_copy(out=b3_f32[:], in_=b3_rows[:])
-            columns_of(b3_cols, b3_f32)
-
-        tanh_bias = const.tile([P, E], F32)
-        ln_bias = const.tile([P, 1], F32)
-
+        raw_rows = const.tile([P, 2, O], F32)
         bound_cols = const.tile([P, P], F32)
-        gap = const.tile([P, 1], F32)
-        gap_tanh = const.tile([P, 1], F32)
-        max_col = bound_cols[:, MAX_ROW : MAX_ROW + 1]
-        min_col = bound_cols[:, MIN_ROW : MIN_ROW + 1]
 
-        def prepare_tanh_bias():
-            raw_rows = const.tile([P, 2, O], F32)
+        def cast_rows():
+            nc.vector.tensor_copy(out=b3_f32[:], in_=b3_rows[:])
             nc.vector.tensor_copy(
                 out=raw_rows[:], in_=bound_rows[:, O:O2].unsqueeze(1).to_broadcast([P, 2, O])
             )
-            columns_of(bound_cols, raw_rows[:].rearrange("p h o -> p (h o)"))
+
+        def transpose_rows():
+            b3_ps = psum_mean.tile([P, P], F32, tag="mean_acc")
+            nc.tensor.transpose(b3_ps[:], b3_f32[:], identity[:])
+            bound_ps = psum_raw.tile([P, P], F32, tag="raw_acc")
+            nc.tensor.transpose(bound_ps[:], raw_rows[:].rearrange("p h o -> p (h o)"), identity[:])
+            return b3_ps, bound_ps
+
+        tanh_bias = const.tile([P, E], F32)
+        half_span = const.tile([P, 1], F32)
+        middle = const.tile([P, 1], F32)
+
+        def prepare_tanh_bias():
             nc.gpsimd.tensor_scalar(
                 out=tanh_bias[:],
                 in0=bound_cols[:, 0:E],
-                scalar1=max_col,
+                scalar1=bound_cols[:, MAX_ROW : MAX_ROW + 1],
                 scalar2=0.5,
                 op0=ALU.subtract,
                 op1=ALU.mult,
             )
-            nc.gpsimd.tensor_tensor(out=gap[:], in0=min_col, in1=max_col, op=ALU.subtract)
 
-        def prepare_ln_bias():
+        def prepare_exps():
+            t = const.tile([P, 2], F32)
             nc.scalar.activation(
-                out=gap_tanh[:], in_=gap[:], func=ACT.Tanh, scale=0.5 / 2**SQUARINGS
+                out=t[:],
+                in_=bound_cols[:, MAX_ROW : MIN_ROW + 1],
+                func=ACT.Tanh,
+                scale=0.5 / 2**SQUARINGS,
             )
-            below = const.tile([P, 1], F32)
+            below = const.tile([P, 2], F32)
             nc.gpsimd.tensor_scalar(
-                out=below[:], in0=gap_tanh[:], scalar1=-1.0, scalar2=1.0, op0=ALU.mult, op1=ALU.add
+                out=below[:], in0=t[:], scalar1=-1.0, scalar2=1.0, op0=ALU.mult, op1=ALU.add
             )
-            above = const.tile([P, 1], F32)
+            above = const.tile([P, 2], F32)
             nc.vector.reciprocal(out=above[:], in_=below[:])
-            power = const.tile([P, 1], F32)
-            nc.gpsimd.tensor_scalar_add(power[:], gap_tanh[:], 1.0)
+            power = const.tile([P, 2], F32)
+            nc.gpsimd.tensor_scalar_add(power[:], t[:], 1.0)
             nc.gpsimd.tensor_tensor(out=power[:], in0=power[:], in1=above[:], op=ALU.mult)
             for i in range(SQUARINGS):
                 nc.gpsimd.tensor_tensor(out=power[:], in0=power[:], in1=power[:], op=ALU.mult)
-            nc.gpsimd.tensor_scalar_add(ln_bias[:], power[:], 0.5)
+            nc.gpsimd.tensor_scalar_mul(half_span[:], power[:, 0:1], 0.5)
+            nc.gpsimd.tensor_tensor(out=middle[:], in0=half_span[:], in1=power[:, 1:2], op=ALU.add)
 
         mean_shift = const.tile([P, E, O], F32)
-        max_spread = const.tile([P, O], F32)
 
         def spread_vectors():
-            spread_ps = psum_mean.tile([P, E + 1, O], F32, tag="mean_ps")
-            for j in range(E + 1):
+            spread_ps = psum_mean.tile([P, E, O], F32, tag="mean_acc")
+            for e in range(E):
                 nc.tensor.matmul(
-                    out=spread_ps[:, j, :],
-                    lhsT=row_picker[:, j : j + 1].to_broadcast([P, P]),
-                    rhs=bound_rows[:, O:O2] if j == MAX_ROW else bound_rows[:, 0:O],
+                    out=spread_ps[:, e, :],
+                    lhsT=row_picker[:, e : e + 1].to_broadcast([P, P]),
+                    rhs=bound_rows[:, 0:O],
                     start=True,
                     stop=True,
                 )
-            nc.vector.tensor_copy(out=mean_shift[:], in_=spread_ps[:, 0:E, :])
-            nc.vector.tensor_copy(out=max_spread[:], in_=spread_ps[:, MAX_ROW, :])
+            nc.vector.tensor_copy(out=mean_shift[:], in_=spread_ps[:])
 
         MEAN_COLS = slice(0, O)
         RAW_HALF = (slice(2 * O, 4 * O), slice(O, 3 * O))
@@ -208,7 +206,8 @@ def tile_ensembledynamicsmodel_pa_kernel(
                 in_=src.rearrange("p t (c i) -> p c t i", i=4),
             )
 
-        W3_PARTS = [slice(n, n + H // HEAD_PARTS) for n in range(0, H, H // HEAD_PARTS)]
+        def w3_parts(count):
+            return [slice(n, n + H // count) for n in range(0, H, H // count)]
 
         def new_w3(e):
             w3_grouped = w_grouped.tile([P, H, PACK], BF16, align_bytes=64)
@@ -217,12 +216,10 @@ def tile_ensembledynamicsmodel_pa_kernel(
             w3_scales = w_mx.tile([P, H], U8, align_bytes=64)
             w3_mx[e] = (w3_codes, w3_scales)
 
-        def regroup_w3(e, part):
-            raw = w3_raw[e]
-            source = raw[part][:] if len(raw) > 1 else raw[0][:, :, :, W3_PARTS[part]]
+        def regroup_w3(e, cols):
             regroup(
-                w3_regrouped[e][:, W3_PARTS[part], :],
-                source.rearrange("p u i n -> p (u i) n"),
+                w3_regrouped[e][:, cols, :],
+                w3_raw[e][:].rearrange("p u (i n) -> p (u i) n", i=2)[:, :, cols],
             )
 
         def quantise_w3(e, cols=slice(0, H)):
@@ -249,6 +246,10 @@ def tile_ensembledynamicsmodel_pa_kernel(
             )
             w4_mx[e] = (w4_codes, w4_scales)
 
+        groups = [(i, PAIR) for i in range(0, N_CHUNKS - SINGLES, PAIR)] + [
+            (i, 1) for i in range(N_CHUNKS - SINGLES, N_CHUNKS)
+        ]
+        group_of = {i: g for g, (first, size) in enumerate(groups) for i in range(first, first + size)}
         h2_t = {}
         h2_grouped = {}
         h2_mx = {}
@@ -280,7 +281,7 @@ def tile_ensembledynamicsmodel_pa_kernel(
             grouped = stage.tile([P, CHUNK * PACK], BF16, align_bytes=64, tag="h2_grouped")
             grouped_words = grouped[:].bitcast(F32)
             for b in range(2):
-                on_vector = i == 1 or b == 1 and (i == 0 or i % CHUNKS_PER_MEMBER in VECTOR_COPIES)
+                on_vector = b == 1 and (i == 1 or VECTOR_COPIES(i))
                 (nc.vector.tensor_copy if on_vector else nc.scalar.copy)(
                     out=grouped_words[:, b * CHUNK : (b + 1) * CHUNK].rearrange(
                         "p (j c u) -> p j c u", j=2, u=2
@@ -295,11 +296,11 @@ def tile_ensembledynamicsmodel_pa_kernel(
             nc.vector.quantize_mx(out=codes[:].bitcast(FP8X4), scales=scales[:], in_=grouped)
             return codes, scales
 
-        def first_product(i):
+        def first_product(i, planes=range(PACK)):
             w3_codes, w3_scales = w3_mx[i // CHUNKS_PER_MEMBER]
             h2_codes, h2_scales = h2_mx[i]
-            banks = []
-            for t in range(PACK):
+            banks = h3_ps.setdefault(i, [])
+            for t in planes:
                 features = slice(t * P, (t + 1) * P)
                 acc = psum_1.tile([P, CHUNK], F32)
                 nc.tensor.matmul_mx(
@@ -312,47 +313,66 @@ def tile_ensembledynamicsmodel_pa_kernel(
                     stop=True,
                 )
                 banks.append(acc)
-            h3_ps[i] = banks
 
-        def silu_h3(i):
+        def silu_h3(i, planes_now=range(PACK)):
             e = i // CHUNKS_PER_MEMBER
-            planes = stage.tile([P, PACK, CHUNK], BF16, tag="h3_planes")
-            for t in range(PACK):
+            group = group_of[i]
+            first, size = groups[group]
+            if i == first and 0 in planes_now:
+                planes = h3_in.tile([P, PACK, size * CHUNK], BF16, tag="planes")
+                h3_planes[group] = planes
+            cols = slice((i - first) * CHUNK, (i - first + 1) * CHUNK)
+            for t in planes_now:
                 nc.scalar.activation(
-                    out=planes[:, t, :],
+                    out=h3_planes[group][:, t, cols],
                     in_=h3_ps[i][t][:],
                     func=ACT.Silu,
                     bias=b3_cols[:, e * PACK + t : e * PACK + t + 1],
                 )
-            h3_planes[i] = planes
 
-        def regroup_h3(i):
-            grouped = stage.tile([P, CHUNK, PACK], BF16, align_bytes=64, tag="h3_grouped")
-            regroup(grouped[:], h3_planes[i][:])
-            h3_grouped[i] = grouped
+        def regroup_h3(group):
+            size = groups[group][1]
+            grouped = h3_stage.tile([P, size * CHUNK, PACK], BF16, align_bytes=64, tag="grouped")
+            regroup(grouped[:], h3_planes[group][:])
+            h3_grouped[group] = grouped
 
-        def second_product(i):
-            w4_codes, w4_scales = w4_mx[i // CHUNKS_PER_MEMBER]
-            h3_codes, h3_scales = h3_mx[i]
-            pair, half = i // PAIR, i % PAIR
-            if half == 0:
-                mean_acc = psum_mean.tile([P, PAIR_ROWS, O], F32, tag="mean_ps")
-                raw_acc = psum_raw.tile([P, CHUNK], F32)
-                mean_ps[pair] = mean_acc
-                raw_ps[pair] = raw_acc
-            nc.tensor.matmul_mx(
-                out=raw_ps[pair][:],
-                lhsT=w4_codes[:, RAW_HALF[half]].bitcast(FP8X4),
-                lhsT_scale=w4_scales[:, RAW_HALF[half]],
-                rhs=h3_codes[:].bitcast(FP8X4),
-                rhs_scale=h3_scales[:],
-                start=(half == 0),
-                stop=(half == PAIR - 1),
+        def quantise_h3(group):
+            size = groups[group][1]
+            codes = h3_stage.tile([P, size * CHUNK], U32, align_bytes=64, tag="codes")
+            scales = h3_stage.tile([P, size * CHUNK], U8, align_bytes=64, tag="scales")
+            nc.vector.quantize_mx(
+                out=codes[:].bitcast(FP8X4),
+                scales=scales[:],
+                in_=h3_grouped[group][:].rearrange("p c t -> p (c t)"),
             )
-            for r in range(TILES):
+            h3_mx[group] = (codes, scales)
+
+        def second_product(group):
+            first, size = groups[group]
+            w4_codes, w4_scales = w4_mx[first // CHUNKS_PER_MEMBER]
+            h3_codes, h3_scales = h3_mx[group]
+            pair = first // PAIR
+            if first % PAIR == 0:
+                raw_acc = psum_raw.tile([P, CHUNK], F32)
+                raw_ps[pair] = raw_acc
+                mean_acc = psum_mean.tile([P, PAIR_ROWS, O], F32)
+                mean_ps[pair] = mean_acc
+            for j in range(size):
+                half = (first + j) % PAIR
+                cols = slice(j * CHUNK, (j + 1) * CHUNK)
+                nc.tensor.matmul_mx(
+                    out=raw_ps[pair][:],
+                    lhsT=w4_codes[:, RAW_HALF[half]].bitcast(FP8X4),
+                    lhsT_scale=w4_scales[:, RAW_HALF[half]],
+                    rhs=h3_codes[:, cols].bitcast(FP8X4),
+                    rhs_scale=h3_scales[:, cols],
+                    start=(half == 0),
+                    stop=(half == PAIR - 1),
+                )
+            for r in range(size * TILES):
                 rows = slice(r * P, (r + 1) * P)
                 nc.tensor.matmul_mx(
-                    out=mean_ps[pair][:, half * TILES + r, :],
+                    out=mean_ps[pair][:, first % PAIR * TILES + r, :],
                     lhsT=h3_codes[:, rows].bitcast(FP8X4),
                     lhsT_scale=h3_scales[:, rows],
                     rhs=w4_codes[:, MEAN_COLS].bitcast(FP8X4),
@@ -374,14 +394,47 @@ def tile_ensembledynamicsmodel_pa_kernel(
             if h == 0:
                 mean_member = outs.tile([P, ROWS_PER_PARTITION, O], F32)
                 mean_sb[e] = mean_member
+            rows = slice(h * PAIR_ROWS, (h + 1) * PAIR_ROWS)
             nc.vector.tensor_tensor(
-                out=mean_sb[e][:, h * PAIR_ROWS : (h + 1) * PAIR_ROWS, :],
+                out=mean_sb[e][:, rows, :],
                 in0=mean_ps[pair][:],
                 in1=mean_shift[:, e, :].unsqueeze(1).to_broadcast([P, PAIR_ROWS, O]),
                 op=ALU.add,
             )
-            if (h + 1) * PAIR == CHUNKS_PER_MEMBER:
-                nc.sync.dma_start(out=mean_rows[e], in_=mean_sb[e][:])
+            nc.sync.dma_start(out=mean_rows[e][:, rows, :], in_=mean_sb[e][:, rows, :])
+
+        def logarithm(pair):
+            nc.scalar.activation(
+                out=tanh_sb[pair][:],
+                in_=tanh_sb[pair][:],
+                func=ACT.Ln,
+                bias=middle[:],
+                scale=half_span[:],
+            )
+
+        def stretch(pair):
+            nc.vector.tensor_scalar(
+                out=tanh_sb[pair][:],
+                in0=tanh_sb[pair][:],
+                scalar1=half_span[:],
+                scalar2=middle[:],
+                op0=ALU.mult,
+                op1=ALU.add,
+            )
+
+        def finish(pair, leave):
+            acc = psum_1.tile([P, TILES, PAIR, O], F32)
+            for r in range(TILES):
+                nc.tensor.transpose(
+                    acc[:, r, :, :].rearrange("p a o -> p (a o)"),
+                    tanh_sb[pair][:, r * P : (r + 1) * P],
+                    identity[:],
+                )
+            e, h = divmod(pair, CHUNKS_PER_MEMBER // PAIR)
+            logvar_pair = logs.tile([P, PAIR_ROWS, O], F32)
+            leave(out=logvar_pair[:].rearrange("p (a r) o -> p r a o", a=PAIR), in_=acc[:])
+            rows = slice(h * PAIR_ROWS, (h + 1) * PAIR_ROWS)
+            nc.sync.dma_start(out=logvar_rows[e][:, rows, :], in_=logvar_pair[:])
 
         def first_chunk_of_member(i):
             return live(i) and i % CHUNKS_PER_MEMBER == 0
@@ -390,86 +443,94 @@ def tile_ensembledynamicsmodel_pa_kernel(
             def quantise_h2(i):
                 h2_mx[i] = quantise(h2_grouped[i][:], "h2")
 
+            parts = w3_parts(PACK)
+            new_w3(0)
+            for cols in parts[:2]:
+                regroup_w3(0, cols)
+            for cols in parts[:2]:
+                quantise_w3(0, cols)
             transpose_h2(0)
             copy_h2(0)
-            new_w3(0)
-            regroup_w3(0, 0)
-            quantise_w3(0, W3_PARTS[0])
-            transpose_b3()
+            cast_rows()
             quantise_h2(0)
-            regroup_w3(0, 1)
-            quantise_w3(0, W3_PARTS[1])
-            first_product(0)
+            b3_ps, bound_ps = transpose_rows()
+            nc.vector.tensor_copy(out=b3_cols[:], in_=b3_ps[:])
+            for cols in parts[2:]:
+                regroup_w3(0, cols)
+            for cols in parts[2:]:
+                quantise_w3(0, cols)
+            nc.vector.tensor_copy(out=bound_cols[:], in_=bound_ps[:])
+            first_product(0, range(2))
             transpose_h2(1)
+            first_product(0, range(2, PACK))
+            silu_h3(0, range(2))
             copy_h2(1)
             quantise_h2(1)
-            silu_h3(0)
+            silu_h3(0, range(2, PACK))
             transpose_h2(2)
+            spread_vectors()
             first_product(1)
             regroup_w4(0)
             quantise_w4(0)
-            for s in range(N_CHUNKS + 1):
-                if live(s + 2):
-                    copy_h2(s + 2)
-                if live(s - 1) and s % PAIR == 0:
-                    tanh_raw((s - 1) // PAIR)
+
+            def take_ln(out, in_):
+                nc.scalar.activation(out=out, in_=in_, func=ACT.Ln, bias=zero[:])
+
+            W = {}
+            for e in range(1, E):
+                a, b, c, d = WSTEP
+                W.setdefault(max(4 * e - 2 - a, 0), []).append((new_w3, e))
+                for lead, f in ((a, lambda e: regroup_w3(e, w3_parts(2)[0])), (b, lambda e: regroup_w3(e, w3_parts(2)[1])), (c, quantise_w3)):
+                    W.setdefault(max(4 * e - 2 - lead, 0), []).append((f, e))
+                W.setdefault(max(4 * e + 2 - d, 0), []).append((lambda e: (regroup_w4(e), quantise_w4(e)), e))
+            RS, QS, MS, TS = {}, {}, {}, {}
+            for g, (first, size) in enumerate(groups):
+                last = first + size - 1
+                r = last - 1 + LAG if size == 2 else last
+                q = r + 1 if size == 2 else r
+                RS.setdefault(r, []).append(g)
+                QS.setdefault(q, []).append(g)
+                if last % 2 == 1:
+                    MS.setdefault(q + 1, []).append(last // 2)
+                    TS.setdefault(q + 1, []).append(last // 2)
+            for s in range(N_CHUNKS + 8):
+                if live(s + LOOK):
+                    copy_h2(s + LOOK)
+                for p in TS.pop(s, ()):
+                    tanh_raw(p)
                 if live(s + 1):
                     silu_h3(s + 1)
-                if live(s):
-                    regroup_h3(s)
-                if live(s + 2):
-                    quantise_h2(s + 2)
-                if live(s):
-                    h3_mx[s] = quantise(h3_grouped[s][:].rearrange("p c t -> p (c t)"), "h3")
-                if live(s - 1) and s % PAIR == 0:
-                    shift_mean((s - 1) // PAIR)
+                for g in RS.get(s, ()):
+                    regroup_h3(g)
+                    if groups[g][1] == 2 and live(s + LOOK):
+                        pass
+                for g in QS.get(s, ()):
+                    if groups[g][1] == 2:
+                        quantise_h3(g)
+                if live(s + LOOK):
+                    quantise_h2(s + LOOK)
+                for p in MS.pop(s, ()):
+                    shift_mean(p)
+                for g in QS.get(s, ()):
+                    if groups[g][1] == 1:
+                        quantise_h3(g)
                 if s == 0:
-                    spread_vectors()
                     prepare_tanh_bias()
                 if s == 3:
-                    prepare_ln_bias()
-                e, stage_of_weights = divmod(s + WEIGHTS_LEAD, CHUNKS_PER_MEMBER)
-                if 0 < e < E:
-                    if stage_of_weights == 0:
-                        new_w3(e)
-                        regroup_w3(e, 0)
-                    elif stage_of_weights == 1:
-                        if e == 1:
-                            new_w3(e)
-                            regroup_w3(e, 0)
-                        regroup_w3(e, 1)
-                    elif stage_of_weights == 2:
-                        quantise_w3(e)
-                    else:
-                        regroup_w4(e)
-                        quantise_w4(e)
-                if live(s + 3):
-                    transpose_h2(s + 3)
-                if live(s):
-                    second_product(s)
+                    prepare_exps()
+                for f, e in W.pop(s, ()):
+                    f(e)
+                if live(s + LOOK + 1):
+                    transpose_h2(s + LOOK + 1)
+                for g in QS.get(s, ()):
+                    second_product(g)
                 if live(s + 2):
                     first_product(s + 2)
-
-            for pair in range(N_PAIRS):
-                nc.scalar.activation(
-                    out=tanh_sb[pair][:], in_=tanh_sb[pair][:], func=ACT.Ln, bias=ln_bias[:], scale=0.5
-                )
-                acc = psum_1.tile([P, TILES, PAIR, O], F32)
-                for r in range(TILES):
-                    nc.tensor.transpose(
-                        acc[:, r, :, :].rearrange("p a o -> p (a o)"),
-                        tanh_sb[pair][:, r * P : (r + 1) * P],
-                        identity[:],
-                    )
-                e, h = divmod(pair, CHUNKS_PER_MEMBER // PAIR)
-                if h == 0:
-                    logvar_member = outs.tile([P, ROWS_PER_PARTITION, O], F32)
-                    logvar_sb[e] = logvar_member
-                rows = slice(h * PAIR_ROWS, (h + 1) * PAIR_ROWS)
-                nc.vector.tensor_tensor(
-                    out=logvar_sb[e][:, rows, :].rearrange("p (a r) o -> p r a o", a=PAIR),
-                    in0=acc[:],
-                    in1=max_spread[:].unsqueeze(1).unsqueeze(1).to_broadcast([P, TILES, PAIR, O]),
-                    op=ALU.add,
-                )
-                nc.sync.dma_start(out=logvar_rows[e][:, rows, :], in_=logvar_sb[e][:, rows, :])
+            zero = const.tile([P, 1], F32)
+            nc.scalar.activation(
+                out=zero[:], in_=tanh_sb[N_PAIRS - 1][:, 0:1], func=ACT.Ln, bias=1.0, scale=0.0
+            )
+            for q in range(N_PAIRS):
+                stretch(q)
+            for q in range(N_PAIRS):
+                finish(q, take_ln)

@@ -202,8 +202,8 @@ def tile_ensembledynamicsmodel_pa_kernel(
 
         def regroup(dst, src):
             nc.vector.tensor_copy(
-                out=dst.rearrange("p (c i) t -> p c t i", i=4),
-                in_=src.rearrange("p t (c i) -> p c t i", i=4),
+                out=dst.rearrange("p (c i) t -> p c t i", i=8),
+                in_=src.rearrange("p t (c i) -> p c t i", i=8),
             )
 
         def w3_parts(count):

@@ -29,11 +29,12 @@ N_PAIRS = N_CHUNKS // PAIR
 PAIR_ROWS = PAIR * TILES
 SQUARINGS = 3
 HEAD_PARTS = 2
-VECTOR_COPIES = lambda i: i%4==1
+VECTOR_COPIES = lambda i: i in (5,9,13,16,17)
 LOOK = 2
 LAG = 1
 SINGLES = 2
-WSTEP = (4, 4, 3, 2)
+LAST_MEANS = 2
+WSTEP = (5, 4, 3, 2)
 SPREAD_STEP = -1
 
 
@@ -56,7 +57,7 @@ def tile_ensembledynamicsmodel_pa_kernel(
         name="stage", bufs=LOOK + 1
     ) as stage, tc.tile_pool(name="h3_in", bufs=3) as h3_in, tc.tile_pool(
         name="h3_stage", bufs=2
-    ) as h3_stage, tc.tile_pool(name="logs", bufs=5) as logs, tc.tile_pool(name="tanhs", bufs=N_PAIRS) as tanhs, tc.tile_pool(
+    ) as h3_stage, tc.tile_pool(name="tanhs", bufs=N_PAIRS) as tanhs, tc.tile_pool(
         name="outs", bufs=2
     ) as outs, tc.psum_pool(name="psum_t", bufs=2) as psum_t, tc.psum_pool(
         name="psum_1", bufs=4
@@ -97,14 +98,14 @@ def tile_ensembledynamicsmodel_pa_kernel(
 
         b3_rows = const.tile([P, P], BF16)
         nc.vector.memset(b3_rows[:], 0.0)
-        nc.scalar.dma_start(
-            out=b3_rows[0 : E * PACK, :], in_=b3.rearrange("e o (t p) -> (e o t) p", p=P)
-        )
         MAX_ROW, MIN_ROW = E, E + 1
         bound_rows = const.tile([P, O2], BF16)
         nc.vector.memset(bound_rows[:], 0.0)
 
         load_w3(0)
+        b3_in = b3.rearrange("e o (t p) -> (e o t) p", p=P)
+        for lo, hi in ((0, 16), (16, E * PACK)):
+            nc.sync.dma_start(out=b3_rows[lo:hi, :], in_=b3_in[lo:hi, :])
         load_chunk(0, parts=HEAD_PARTS)
         nc.sync.dma_start(out=bound_rows[0:E, :], in_=b4.rearrange("e o n -> (e o) n"))
         nc.sync.dma_start(out=bound_rows[MAX_ROW : MAX_ROW + 1, O:O2], in_=max_logvar)
@@ -112,10 +113,10 @@ def tile_ensembledynamicsmodel_pa_kernel(
         load_chunk(1)
         load_w4(0)
         for i in range(2, H2_BUFS):
+            load_chunk(i)
             if i - 1 < E:
                 load_w3(i - 1)
                 load_w4(i - 1)
-            load_chunk(i)
 
         warm_input = const.tile([P, 1], F32)
         nc.vector.memset(warm_input[:], 1.0)
@@ -127,18 +128,23 @@ def tile_ensembledynamicsmodel_pa_kernel(
         raw_rows = const.tile([P, 2, O], F32)
         bound_cols = const.tile([P, P], F32)
 
-        def cast_rows():
-            nc.vector.tensor_copy(out=b3_f32[:], in_=b3_rows[:])
-            nc.vector.tensor_copy(
+        def cast_b3():
+            nc.gpsimd.tensor_copy(out=b3_f32[:], in_=b3_rows[:])
+
+        def cast_bounds():
+            nc.gpsimd.tensor_copy(
                 out=raw_rows[:], in_=bound_rows[:, O:O2].unsqueeze(1).to_broadcast([P, 2, O])
             )
 
-        def transpose_rows():
+        def transpose_b3():
             b3_ps = psum_mean.tile([P, P], F32, tag="mean_acc")
             nc.tensor.transpose(b3_ps[:], b3_f32[:], identity[:])
+            return b3_ps
+
+        def transpose_bounds():
             bound_ps = psum_raw.tile([P, P], F32, tag="raw_acc")
             nc.tensor.transpose(bound_ps[:], raw_rows[:].rearrange("p h o -> p (h o)"), identity[:])
-            return b3_ps, bound_ps
+            return bound_ps
 
         tanh_bias = const.tile([P, E], F32)
         half_span = const.tile([P, 1], F32)
@@ -154,18 +160,21 @@ def tile_ensembledynamicsmodel_pa_kernel(
                 op1=ALU.mult,
             )
 
+        t = const.tile([P, 2], F32)
+        below = const.tile([P, 2], F32)
+
         def prepare_exps():
-            t = const.tile([P, 2], F32)
             nc.scalar.activation(
                 out=t[:],
                 in_=bound_cols[:, MAX_ROW : MIN_ROW + 1],
                 func=ACT.Tanh,
                 scale=0.5 / 2**SQUARINGS,
             )
-            below = const.tile([P, 2], F32)
             nc.gpsimd.tensor_scalar(
                 out=below[:], in0=t[:], scalar1=-1.0, scalar2=1.0, op0=ALU.mult, op1=ALU.add
             )
+
+        def finish_exps():
             above = const.tile([P, 2], F32)
             nc.vector.reciprocal(out=above[:], in_=below[:])
             power = const.tile([P, 2], F32)
@@ -263,69 +272,77 @@ def tile_ensembledynamicsmodel_pa_kernel(
         tanh_sb = {}
         logvar_sb = {}
 
-        def transpose_h2(i):
+        def transpose_h2(i, banks=(0, 1)):
             words = h2_raw[i][:].bitcast(F32)
-            banks = []
-            for b in range(2):
+            for b in banks:
                 xt = psum_t.tile([P, 2, 2, P], F32)
                 for j in range(2):
                     for u in range(2):
                         first = (2 * b + j) * (H // 2) + u * P
                         nc.tensor.transpose(xt[:, j, u, :], words[:, first : first + P], identity[:])
-                banks.append(xt)
-            h2_t[i] = banks
-            if live(i + H2_BUFS):
+                h2_t[i, b] = xt
+            if 1 in banks and live(i + H2_BUFS):
                 load_chunk(i + H2_BUFS)
 
-        def copy_h2(i):
-            grouped = stage.tile([P, CHUNK * PACK], BF16, align_bytes=64, tag="h2_grouped")
-            grouped_words = grouped[:].bitcast(F32)
-            for b in range(2):
+        def copy_h2(i, banks=(0, 1)):
+            if 0 in banks:
+                grouped = stage.tile([P, CHUNK * PACK], BF16, align_bytes=64, tag="h2_grouped")
+                h2_grouped[i] = grouped
+            grouped_words = h2_grouped[i][:].bitcast(F32)
+            for b in banks:
                 on_vector = b == 1 and (i == 1 or VECTOR_COPIES(i))
                 (nc.vector.tensor_copy if on_vector else nc.scalar.copy)(
                     out=grouped_words[:, b * CHUNK : (b + 1) * CHUNK].rearrange(
                         "p (j c u) -> p j c u", j=2, u=2
                     ),
-                    in_=h2_t[i][b][:].rearrange("p j u c -> p j c u"),
+                    in_=h2_t[i, b][:].rearrange("p j u c -> p j c u"),
                 )
-            h2_grouped[i] = grouped
 
-        def quantise(grouped, tag):
-            codes = stage.tile([P, CHUNK], U32, align_bytes=64, tag=tag + "_codes")
-            scales = stage.tile([P, CHUNK], U8, align_bytes=64, tag=tag + "_scales")
-            nc.vector.quantize_mx(out=codes[:].bitcast(FP8X4), scales=scales[:], in_=grouped)
-            return codes, scales
+        WHOLE = slice(0, CHUNK)
+        HALVES = (slice(0, CHUNK // 2), slice(CHUNK // 2, CHUNK))
 
-        def first_product(i, planes=range(PACK)):
+        def quantise_h2(i, cols=WHOLE):
+            if cols.start == 0:
+                codes = stage.tile([P, CHUNK], U32, align_bytes=64, tag="h2_codes")
+                scales = stage.tile([P, CHUNK], U8, align_bytes=64, tag="h2_scales")
+                h2_mx[i] = (codes, scales)
+            codes, scales = h2_mx[i]
+            nc.vector.quantize_mx(
+                out=codes[:, cols].bitcast(FP8X4),
+                scales=scales[:, cols],
+                in_=h2_grouped[i][:, cols.start * PACK : cols.stop * PACK],
+            )
+
+        def first_product(i, planes=range(PACK), cols=WHOLE):
             w3_codes, w3_scales = w3_mx[i // CHUNKS_PER_MEMBER]
             h2_codes, h2_scales = h2_mx[i]
-            banks = h3_ps.setdefault(i, [])
             for t in planes:
                 features = slice(t * P, (t + 1) * P)
-                acc = psum_1.tile([P, CHUNK], F32)
+                if cols.start == 0:
+                    acc = psum_1.tile([P, CHUNK], F32)
+                    h3_ps[i, t] = acc
                 nc.tensor.matmul_mx(
-                    out=acc[:],
+                    out=h3_ps[i, t][:, cols],
                     lhsT=w3_codes[:, features].bitcast(FP8X4),
                     lhsT_scale=w3_scales[:, features],
-                    rhs=h2_codes[:].bitcast(FP8X4),
-                    rhs_scale=h2_scales[:],
+                    rhs=h2_codes[:, cols].bitcast(FP8X4),
+                    rhs_scale=h2_scales[:, cols],
                     start=True,
                     stop=True,
                 )
-                banks.append(acc)
 
-        def silu_h3(i, planes_now=range(PACK)):
+        def silu_h3(i, planes_now=range(PACK), cols=WHOLE):
             e = i // CHUNKS_PER_MEMBER
             group = group_of[i]
             first, size = groups[group]
-            if i == first and 0 in planes_now:
+            if group not in h3_planes:
                 planes = h3_in.tile([P, PACK, size * CHUNK], BF16, tag="planes")
                 h3_planes[group] = planes
-            cols = slice((i - first) * CHUNK, (i - first + 1) * CHUNK)
+            at = (i - first) * CHUNK
             for t in planes_now:
                 nc.scalar.activation(
-                    out=h3_planes[group][:, t, cols],
-                    in_=h3_ps[i][t][:],
+                    out=h3_planes[group][:, t, at + cols.start : at + cols.stop],
+                    in_=h3_ps[i, t][:, cols],
                     func=ACT.Silu,
                     bias=b3_cols[:, e * PACK + t : e * PACK + t + 1],
                 )
@@ -355,7 +372,10 @@ def tile_ensembledynamicsmodel_pa_kernel(
             if first % PAIR == 0:
                 raw_acc = psum_raw.tile([P, CHUNK], F32)
                 raw_ps[pair] = raw_acc
-                mean_acc = psum_mean.tile([P, PAIR_ROWS, O], F32)
+                if pair < N_PAIRS - LAST_MEANS:
+                    mean_acc = psum_mean.tile([P, PAIR_ROWS, O], F32)
+                else:
+                    mean_acc = psum_t.tile([P, PAIR_ROWS, O], F32, tag="xt")
                 mean_ps[pair] = mean_acc
             for j in range(size):
                 half = (first + j) % PAIR
@@ -431,45 +451,46 @@ def tile_ensembledynamicsmodel_pa_kernel(
                     identity[:],
                 )
             e, h = divmod(pair, CHUNKS_PER_MEMBER // PAIR)
-            logvar_pair = logs.tile([P, PAIR_ROWS, O], F32)
-            leave(out=logvar_pair[:].rearrange("p (a r) o -> p r a o", a=PAIR), in_=acc[:])
-            rows = slice(h * PAIR_ROWS, (h + 1) * PAIR_ROWS)
-            nc.sync.dma_start(out=logvar_rows[e][:, rows, :], in_=logvar_pair[:])
+            logvar_pair = tanh_sb[pair][:].rearrange("p (a r o) -> p a r o", a=PAIR, r=TILES)
+            for a in (slice(0, PAIR),) if pair < N_PAIRS - 1 else (slice(0, 1), slice(1, 2)):
+                leave(out=logvar_pair[:, a].rearrange("p a r o -> p r a o"), in_=acc[:, :, a, :])
+                rows = slice(h * PAIR_ROWS + a.start * TILES, h * PAIR_ROWS + a.stop * TILES)
+                nc.sync.dma_start(
+                    out=logvar_rows[e][:, rows, :],
+                    in_=logvar_pair[:, a].rearrange("p a r o -> p (a r) o"),
+                )
 
         def first_chunk_of_member(i):
             return live(i) and i % CHUNKS_PER_MEMBER == 0
 
         with tc.manual_schedule():
-            def quantise_h2(i):
-                h2_mx[i] = quantise(h2_grouped[i][:], "h2")
-
             parts = w3_parts(PACK)
             new_w3(0)
             for cols in parts[:2]:
                 regroup_w3(0, cols)
+            cast_b3()
             for cols in parts[:2]:
                 quantise_w3(0, cols)
             transpose_h2(0)
             copy_h2(0)
-            cast_rows()
-            quantise_h2(0)
-            b3_ps, bound_ps = transpose_rows()
-            nc.vector.tensor_copy(out=b3_cols[:], in_=b3_ps[:])
+            b3_ps = transpose_b3()
+            nc.scalar.copy(out=b3_cols[:], in_=b3_ps[:])
+            for cols in HALVES:
+                quantise_h2(0, cols)
+                first_product(0, range(2), cols)
+                silu_h3(0, range(2), cols)
             for cols in parts[2:]:
                 regroup_w3(0, cols)
             for cols in parts[2:]:
                 quantise_w3(0, cols)
-            nc.vector.tensor_copy(out=bound_cols[:], in_=bound_ps[:])
-            first_product(0, range(2))
             transpose_h2(1)
             first_product(0, range(2, PACK))
-            silu_h3(0, range(2))
             copy_h2(1)
             quantise_h2(1)
             silu_h3(0, range(2, PACK))
             transpose_h2(2)
-            spread_vectors()
             first_product(1)
+            cast_bounds()
             regroup_w4(0)
             quantise_w4(0)
 
@@ -491,7 +512,8 @@ def tile_ensembledynamicsmodel_pa_kernel(
                 RS.setdefault(r, []).append(g)
                 QS.setdefault(q, []).append(g)
                 if last % 2 == 1:
-                    MS.setdefault(q + 1, []).append(last // 2)
+                    if last // 2 < N_PAIRS - LAST_MEANS:
+                        MS.setdefault(q + 1, []).append(last // 2)
                     TS.setdefault(q + 1, []).append(last // 2)
             for s in range(N_CHUNKS + 8):
                 if live(s + LOOK):
@@ -515,9 +537,14 @@ def tile_ensembledynamicsmodel_pa_kernel(
                     if groups[g][1] == 1:
                         quantise_h3(g)
                 if s == 0:
+                    bound_ps = transpose_bounds()
+                    spread_vectors()
+                    nc.scalar.copy(out=bound_cols[:], in_=bound_ps[:])
                     prepare_tanh_bias()
-                if s == 3:
+                if s == 1:
                     prepare_exps()
+                if s == 3:
+                    finish_exps()
                 for f, e in W.pop(s, ()):
                     f(e)
                 if live(s + LOOK + 1):
@@ -532,5 +559,8 @@ def tile_ensembledynamicsmodel_pa_kernel(
             )
             for q in range(N_PAIRS):
                 stretch(q)
+                if q == 3:
+                    for p in range(N_PAIRS - LAST_MEANS, N_PAIRS):
+                        shift_mean(p)
             for q in range(N_PAIRS):
                 finish(q, take_ln)

@@ -29,11 +29,13 @@ N_PAIRS = N_CHUNKS // PAIR
 PAIR_ROWS = PAIR * TILES
 SQUARINGS = 3
 HEAD_PARTS = 2
-VECTOR_COPIES = lambda i: i in (5,9,13,16,17)
+VECTOR_COPIES = lambda i: i in (2,9,13,16,17)
 LOOK = 2
 LAG = 1
 SINGLES = 2
 LAST_MEANS = 2
+LATE_MEANS = 2
+M7 = 18
 WSTEP = (5, 4, 3, 2)
 SPREAD_STEP = -1
 
@@ -98,14 +100,14 @@ def tile_ensembledynamicsmodel_pa_kernel(
 
         b3_rows = const.tile([P, P], BF16)
         nc.vector.memset(b3_rows[:], 0.0)
+        nc.scalar.dma_start(
+            out=b3_rows[0 : E * PACK, :], in_=b3.rearrange("e o (t p) -> (e o t) p", p=P)
+        )
         MAX_ROW, MIN_ROW = E, E + 1
         bound_rows = const.tile([P, O2], BF16)
         nc.vector.memset(bound_rows[:], 0.0)
 
         load_w3(0)
-        b3_in = b3.rearrange("e o (t p) -> (e o t) p", p=P)
-        for lo, hi in ((0, 16), (16, E * PACK)):
-            nc.sync.dma_start(out=b3_rows[lo:hi, :], in_=b3_in[lo:hi, :])
         load_chunk(0, parts=HEAD_PARTS)
         nc.sync.dma_start(out=bound_rows[0:E, :], in_=b4.rearrange("e o n -> (e o) n"))
         nc.sync.dma_start(out=bound_rows[MAX_ROW : MAX_ROW + 1, O:O2], in_=max_logvar)
@@ -129,10 +131,10 @@ def tile_ensembledynamicsmodel_pa_kernel(
         bound_cols = const.tile([P, P], F32)
 
         def cast_b3():
-            nc.gpsimd.tensor_copy(out=b3_f32[:], in_=b3_rows[:])
+            nc.vector.tensor_copy(out=b3_f32[:], in_=b3_rows[:])
 
         def cast_bounds():
-            nc.gpsimd.tensor_copy(
+            nc.vector.tensor_copy(
                 out=raw_rows[:], in_=bound_rows[:, O:O2].unsqueeze(1).to_broadcast([P, 2, O])
             )
 
@@ -370,12 +372,13 @@ def tile_ensembledynamicsmodel_pa_kernel(
             h3_codes, h3_scales = h3_mx[group]
             pair = first // PAIR
             if first % PAIR == 0:
-                raw_acc = psum_raw.tile([P, CHUNK], F32)
-                raw_ps[pair] = raw_acc
-                if pair < N_PAIRS - LAST_MEANS:
+                if pair != N_PAIRS - 2:
+                    raw_acc = psum_raw.tile([P, CHUNK], F32)
                     mean_acc = psum_mean.tile([P, PAIR_ROWS, O], F32)
                 else:
+                    raw_acc = psum_t.tile([P, CHUNK], F32, tag="xt")
                     mean_acc = psum_t.tile([P, PAIR_ROWS, O], F32, tag="xt")
+                raw_ps[pair] = raw_acc
                 mean_ps[pair] = mean_acc
             for j in range(size):
                 half = (first + j) % PAIR
@@ -468,11 +471,11 @@ def tile_ensembledynamicsmodel_pa_kernel(
             new_w3(0)
             for cols in parts[:2]:
                 regroup_w3(0, cols)
-            cast_b3()
             for cols in parts[:2]:
                 quantise_w3(0, cols)
             transpose_h2(0)
             copy_h2(0)
+            cast_b3()
             b3_ps = transpose_b3()
             nc.scalar.copy(out=b3_cols[:], in_=b3_ps[:])
             for cols in HALVES:
@@ -508,31 +511,42 @@ def tile_ensembledynamicsmodel_pa_kernel(
             for g, (first, size) in enumerate(groups):
                 last = first + size - 1
                 r = last - 1 + LAG if size == 2 else last
-                q = r + 1 if size == 2 else r
+                q = r + 1 if size == 2 and last < N_CHUNKS - 1 - SINGLES else r
                 RS.setdefault(r, []).append(g)
                 QS.setdefault(q, []).append(g)
                 if last % 2 == 1:
-                    if last // 2 < N_PAIRS - LAST_MEANS:
-                        MS.setdefault(q + 1, []).append(last // 2)
+                    if last // 2 < N_PAIRS - LATE_MEANS:
+                        MS.setdefault(q + 1 if last // 2 < N_PAIRS - 3 else M7, []).append(last // 2)
                     TS.setdefault(q + 1, []).append(last // 2)
             for s in range(N_CHUNKS + 8):
                 if live(s + LOOK):
                     copy_h2(s + LOOK)
-                for p in TS.pop(s, ()):
-                    tanh_raw(p)
+                ending = s >= N_CHUNKS - 3
+                if not ending:
+                    for p in TS.pop(s, ()):
+                        tanh_raw(p)
                 if live(s + 1):
                     silu_h3(s + 1)
+                for p in TS.pop(s, ()):
+                    tanh_raw(p)
+                if s == N_CHUNKS - 1:
+                    for p in MS.pop(s, ()):
+                        shift_mean(p)
                 for g in RS.get(s, ()):
                     regroup_h3(g)
                     if groups[g][1] == 2 and live(s + LOOK):
                         pass
                 for g in QS.get(s, ()):
-                    if groups[g][1] == 2:
+                    if groups[g][1] == 2 and g not in RS.get(s, ()):
                         quantise_h3(g)
                 if live(s + LOOK):
                     quantise_h2(s + LOOK)
-                for p in MS.pop(s, ()):
-                    shift_mean(p)
+                for g in QS.get(s, ()):
+                    if groups[g][1] == 2 and g in RS.get(s, ()):
+                        quantise_h3(g)
+                if s != N_CHUNKS - 1:
+                    for p in MS.pop(s, ()):
+                        shift_mean(p)
                 for g in QS.get(s, ()):
                     if groups[g][1] == 1:
                         quantise_h3(g)
@@ -549,18 +563,21 @@ def tile_ensembledynamicsmodel_pa_kernel(
                     f(e)
                 if live(s + LOOK + 1):
                     transpose_h2(s + LOOK + 1)
+                if live(s + 2) and ending:
+                    first_product(s + 2)
                 for g in QS.get(s, ()):
                     second_product(g)
-                if live(s + 2):
+                if live(s + 2) and not ending:
                     first_product(s + 2)
             zero = const.tile([P, 1], F32)
             nc.scalar.activation(
                 out=zero[:], in_=tanh_sb[N_PAIRS - 1][:, 0:1], func=ACT.Ln, bias=1.0, scale=0.0
             )
+            for p in range(N_PAIRS - LATE_MEANS, N_PAIRS - 1):
+                shift_mean(p)
             for q in range(N_PAIRS):
                 stretch(q)
                 if q == 3:
-                    for p in range(N_PAIRS - LAST_MEANS, N_PAIRS):
-                        shift_mean(p)
+                    shift_mean(N_PAIRS - 1)
             for q in range(N_PAIRS):
                 finish(q, take_ln)

@@ -35,6 +35,9 @@ LAG = 1
 SINGLES = 2
 LAST_MEANS = 2
 LATE_MEANS = 2
+HEAD_IDLE = 6
+STEP_IDLE = 3
+MFIRST = False
 M7 = 18
 WSTEP = (5, 4, 3, 2)
 SPREAD_STEP = -1
@@ -100,6 +103,8 @@ def tile_ensembledynamicsmodel_pa_kernel(
 
         b3_rows = const.tile([P, P], BF16)
         nc.vector.memset(b3_rows[:], 0.0)
+        blank = const.tile([P, CHUNK], BF16)
+        nc.vector.memset(blank[:], 0.0)
         nc.scalar.dma_start(
             out=b3_rows[0 : E * PACK, :], in_=b3.rearrange("e o (t p) -> (e o t) p", p=P)
         )
@@ -120,10 +125,16 @@ def tile_ensembledynamicsmodel_pa_kernel(
                 load_w3(i - 1)
                 load_w4(i - 1)
 
-        warm_input = const.tile([P, 1], F32)
-        nc.vector.memset(warm_input[:], 1.0)
         table_warmer = const.tile([P, 1], F32)
-        nc.scalar.activation(out=table_warmer[:], in_=warm_input[:], func=ACT.Silu)
+        nc.scalar.activation(out=table_warmer[:], in_=blank[:, 0:1], func=ACT.Silu)
+
+        def keep_tensor_busy(count):
+            for i in range(count):
+                idle_acc = psum_raw.tile([P, CHUNK], F32, tag="raw_acc")
+                nc.tensor.matmul(
+                    out=idle_acc[:], lhsT=blank[:, 0:P], rhs=blank[:], start=True, stop=True
+                )
+
 
         b3_f32 = const.tile([P, P], F32)
         b3_cols = const.tile([P, P], F32)
@@ -473,6 +484,7 @@ def tile_ensembledynamicsmodel_pa_kernel(
                 regroup_w3(0, cols)
             for cols in parts[:2]:
                 quantise_w3(0, cols)
+            keep_tensor_busy(HEAD_IDLE)
             transpose_h2(0)
             copy_h2(0)
             cast_b3()
@@ -529,7 +541,7 @@ def tile_ensembledynamicsmodel_pa_kernel(
                     silu_h3(s + 1)
                 for p in TS.pop(s, ()):
                     tanh_raw(p)
-                if s == N_CHUNKS - 1:
+                if MFIRST or s == N_CHUNKS - 1:
                     for p in MS.pop(s, ()):
                         shift_mean(p)
                 for g in RS.get(s, ()):
@@ -544,9 +556,8 @@ def tile_ensembledynamicsmodel_pa_kernel(
                 for g in QS.get(s, ()):
                     if groups[g][1] == 2 and g in RS.get(s, ()):
                         quantise_h3(g)
-                if s != N_CHUNKS - 1:
-                    for p in MS.pop(s, ()):
-                        shift_mean(p)
+                for p in MS.pop(s, ()):
+                    shift_mean(p)
                 for g in QS.get(s, ()):
                     if groups[g][1] == 1:
                         quantise_h3(g)
@@ -563,6 +574,8 @@ def tile_ensembledynamicsmodel_pa_kernel(
                     f(e)
                 if live(s + LOOK + 1):
                     transpose_h2(s + LOOK + 1)
+                if s % 2 == 1 and 1 < s < 16:
+                    keep_tensor_busy(STEP_IDLE)
                 if live(s + 2) and ending:
                     first_product(s + 2)
                 for g in QS.get(s, ()):

@@ -129,8 +129,8 @@ def tile_ensembledynamicsmodel_pa_kernel(
         nc.scalar.activation(out=table_warmer[:], in_=blank[:, 0:1], func=ACT.Silu)
 
         def keep_tensor_busy(count):
+            idle_acc = psum_raw.tile([P, CHUNK], F32, tag="raw_acc")
             for i in range(count):
-                idle_acc = psum_raw.tile([P, CHUNK], F32, tag="raw_acc")
                 nc.tensor.matmul(
                     out=idle_acc[:], lhsT=blank[:, 0:P], rhs=blank[:], start=True, stop=True
                 )

import concourse.mybir as mybir
from concourse.masks import make_identity

F32 = mybir.dt.float32
BF16 = mybir.dt.bfloat16
U32 = mybir.dt.uint32
U8 = mybir.dt.uint8
FP8X4 = mybir.dt.float8_e4m3fn_x4
ACT = mybir.ActivationFunctionType
ALU = mybir.AluOpType

E, B, H, O = 5, 2048, 512, 64
O2 = 2 * O
FLOPS = 2 * E * B * H * (H + O2)

P = 128
PACK = 4
assert H == P * PACK

ROWS_PER_PARTITION = B // P
TILES = 4
CHUNK = TILES * P
CHUNKS_PER_MEMBER = B // CHUNK
N_CHUNKS = E * CHUNKS_PER_MEMBER
H2_BUFS = 8
WEIGHTS_LEAD = 5
PAIR = 2
N_PAIRS = N_CHUNKS // PAIR
PAIR_ROWS = PAIR * TILES
SQUARINGS = 3
HEAD_PARTS = 2
VECTOR_COPIES = lambda i: i in (2,9,13,16,17)
LOOK = 2
LAG = 1
SINGLES = 2
LAST_MEANS = 2
LATE_MEANS = 2
HEAD_IDLE = 6
STEP_IDLE = 3
MFIRST = False
M7 = 18
WSTEP = (5, 4, 3, 2)
SPREAD_STEP = -1


def tile_ensembledynamicsmodel_pa_kernel(
    tc, h2, w3, b3, w4, b4, max_logvar, min_logvar, out_0, out_1
):
    nc = tc.nc

    h2_chunks = h2.rearrange("e (p g r) k -> e g p (r k)", g=CHUNKS_PER_MEMBER, r=TILES)
    mean_rows = out_0.rearrange("e (p r) o -> e p r o", r=ROWS_PER_PARTITION)
    logvar_rows = out_1.rearrange("e (p r) o -> e p r o", r=ROWS_PER_PARTITION)
    w3_rows = w3.rearrange("e (u p i) n -> e p u (i n)", u=2, i=2)
    w4_rows = w4.rearrange("e (t p) n -> e p t n", p=P)

    with tc.tile_pool(name="const", bufs=1) as const, tc.tile_pool(
        name="w_raw", bufs=E
    ) as w_raw, tc.tile_pool(name="w_grouped", bufs=2) as w_grouped, tc.tile_pool(
        name="w_mx", bufs=3
    ) as w_mx, tc.tile_pool(name="h2_in", bufs=H2_BUFS) as h2_in, tc.tile_pool(
        name="stage", bufs=LOOK + 1
    ) as stage, tc.tile_pool(name="h3_in", bufs=3) as h3_in, tc.tile_pool(
        name="h3_stage", bufs=2
    ) as h3_stage, tc.tile_pool(name="tanhs", bufs=N_PAIRS) as tanhs, tc.tile_pool(
        name="outs", bufs=2
    ) as outs, tc.psum_pool(name="psum_t", bufs=2) as psum_t, tc.psum_pool(
        name="psum_1", bufs=4
    ) as psum_1, tc.psum_pool(name="psum_mean", bufs=1) as psum_mean, tc.psum_pool(
        name="psum_raw", bufs=1
    ) as psum_raw:
        def live(i):
            return 0 <= i < N_CHUNKS

        h2_raw = {}
        w3_raw = {}
        w4_raw = {}

        def load_w3(e):
            w3_in = w_raw.tile([P, 2, 2 * H], BF16)
            nc.sync.dma_start(out=w3_in[:], in_=w3_rows[e])
            w3_raw[e] = w3_in

        def load_w4(e):
            w4_in = w_raw.tile([P, PACK, O2], BF16)
            nc.sync.dma_start(out=w4_in[:], in_=w4_rows[e])
            w4_raw[e] = w4_in

        def load_chunk(i, parts=1):
            h2_rows = h2_in.tile([P, TILES * H], BF16)
            for at in range(0, TILES * H, TILES * H // parts):
                part = slice(at, at + TILES * H // parts)
                nc.sync.dma_start(
                    out=h2_rows[:, part],
                    in_=h2_chunks[i // CHUNKS_PER_MEMBER, i % CHUNKS_PER_MEMBER][:, part],
                )
            h2_raw[i] = h2_rows

        identity = const.tile([P, P], F32)
        make_identity(nc, identity[:])
        row_picker = const.tile([P, P], BF16)
        make_identity(nc, row_picker[:])

        b3_rows = const.tile([P, P], BF16)
        nc.vector.memset(b3_rows[:], 0.0)
        blank = const.tile([P, CHUNK], BF16)
        nc.vector.memset(blank[:], 0.0)
        nc.scalar.dma_start(
            out=b3_rows[0 : E * PACK, :], in_=b3.rearrange("e o (t p) -> (e o t) p", p=P)
        )
        MAX_ROW, MIN_ROW = E, E + 1
        bound_rows = const.tile([P, O2], BF16)
        nc.vector.memset(bound_rows[:], 0.0)

        load_w3(0)
        load_chunk(0, parts=HEAD_PARTS)
        nc.sync.dma_start(out=bound_rows[0:E, :], in_=b4.rearrange("e o n -> (e o) n"))
        nc.sync.dma_start(out=bound_rows[MAX_ROW : MAX_ROW + 1, O:O2], in_=max_logvar)
        nc.sync.dma_start(out=bound_rows[MIN_ROW : MIN_ROW + 1, O:O2], in_=min_logvar)
        load_chunk(1)
        load_w4(0)
        for i in range(2, H2_BUFS):
            load_chunk(i)
            if i - 1 < E:
                load_w3(i - 1)
                load_w4(i - 1)

        table_warmer = const.tile([P, 1], F32)
        nc.scalar.activation(out=table_warmer[:], in_=blank[:, 0:1], func=ACT.Silu)

        def keep_tensor_busy(count):
            idle_acc = psum_raw.tile([P, CHUNK], F32, tag="raw_acc")
            for i in range(count):
                nc.tensor.matmul(
                    out=idle_acc[:], lhsT=blank[:, 0:P], rhs=blank[:], start=True, stop=True
                )


        b3_f32 = const.tile([P, P], F32)
        b3_cols = const.tile([P, P], F32)
        raw_rows = const.tile([P, 2, O], F32)
        bound_cols = const.tile([P, P], F32)

        def cast_b3():
            nc.vector.tensor_copy(out=b3_f32[:], in_=b3_rows[:])

        def cast_bounds():
            nc.vector.tensor_copy(
                out=raw_rows[:], in_=bound_rows[:, O:O2].unsqueeze(1).to_broadcast([P, 2, O])
            )

        def transpose_b3():
            b3_ps = psum_mean.tile([P, P], F32, tag="mean_acc")
            nc.tensor.transpose(b3_ps[:], b3_f32[:], identity[:])
            return b3_ps

        def transpose_bounds():
            bound_ps = psum_raw.tile([P, P], F32, tag="raw_acc")
            nc.tensor.transpose(bound_ps[:], raw_rows[:].rearrange("p h o -> p (h o)"), identity[:])
            return bound_ps

        tanh_bias = const.tile([P, E], F32)
        half_span = const.tile([P, 1], F32)
        middle = const.tile([P, 1], F32)

        def prepare_tanh_bias():
            nc.gpsimd.tensor_scalar(
                out=tanh_bias[:],
                in0=bound_cols[:, 0:E],
                scalar1=bound_cols[:, MAX_ROW : MAX_ROW + 1],
                scalar2=0.5,
                op0=ALU.subtract,
                op1=ALU.mult,
            )

        t = const.tile([P, 2], F32)
        below = const.tile([P, 2], F32)

        def prepare_exps():
            nc.scalar.activation(
                out=t[:],
                in_=bound_cols[:, MAX_ROW : MIN_ROW + 1],
                func=ACT.Tanh,
                scale=0.5 / 2**SQUARINGS,
            )
            nc.gpsimd.tensor_scalar(
                out=below[:], in0=t[:], scalar1=-1.0, scalar2=1.0, op0=ALU.mult, op1=ALU.add
            )

        def finish_exps():
            above = const.tile([P, 2], F32)
            nc.vector.reciprocal(out=above[:], in_=below[:])
            power = const.tile([P, 2], F32)
            nc.gpsimd.tensor_scalar_add(power[:], t[:], 1.0)
            nc.gpsimd.tensor_tensor(out=power[:], in0=power[:], in1=above[:], op=ALU.mult)
            for i in range(SQUARINGS):
                nc.gpsimd.tensor_tensor(out=power[:], in0=power[:], in1=power[:], op=ALU.mult)
            nc.gpsimd.tensor_scalar_mul(half_span[:], power[:, 0:1], 0.5)
            nc.gpsimd.tensor_tensor(out=middle[:], in0=half_span[:], in1=power[:, 1:2], op=ALU.add)

        mean_shift = const.tile([P, E, O], F32)

        def spread_vectors():
            spread_ps = psum_mean.tile([P, E, O], F32, tag="mean_acc")
            for e in range(E):
                nc.tensor.matmul(
                    out=spread_ps[:, e, :],
                    lhsT=row_picker[:, e : e + 1].to_broadcast([P, P]),
                    rhs=bound_rows[:, 0:O],
                    start=True,
                    stop=True,
                )
            nc.vector.tensor_copy(out=mean_shift[:], in_=spread_ps[:])

        MEAN_COLS = slice(0, O)
        RAW_HALF = (slice(2 * O, 4 * O), slice(O, 3 * O))
        w4_grouped = const.tile([P, E, 4 * O, PACK], BF16, align_bytes=64)
        for zeros in (slice(O, 2 * O), slice(3 * O, 4 * O)):
            nc.vector.memset(w4_grouped[:, :, zeros, :], 0.0)

        w3_regrouped = {}
        w3_mx = {}
        w4_mx = {}

        def regroup(dst, src):
            nc.vector.tensor_copy(
                out=dst.rearrange("p (c i) t -> p c t i", i=8),
                in_=src.rearrange("p t (c i) -> p c t i", i=8),
            )

        def w3_parts(count):
            return [slice(n, n + H // count) for n in range(0, H, H // count)]

        def new_w3(e):
            w3_grouped = w_grouped.tile([P, H, PACK], BF16, align_bytes=64)
            w3_regrouped[e] = w3_grouped
            w3_codes = w_mx.tile([P, H], U32, align_bytes=64)
            w3_scales = w_mx.tile([P, H], U8, align_bytes=64)
            w3_mx[e] = (w3_codes, w3_scales)

        def regroup_w3(e, cols):
            regroup(
                w3_regrouped[e][:, cols, :],
                w3_raw[e][:].rearrange("p u (i n) -> p (u i) n", i=2)[:, :, cols],
            )

        def quantise_w3(e, cols=slice(0, H)):
            w3_codes, w3_scales = w3_mx[e]
            nc.vector.quantize_mx(
                out=w3_codes[:, cols].bitcast(FP8X4),
                scales=w3_scales[:, cols],
                in_=w3_regrouped[e][:, cols, :].rearrange("p c t -> p (c t)"),
            )

        def regroup_w4(e):
            nc.vector.tensor_copy(
                out=w4_grouped[:, e].rearrange("p (h c) t -> p h c t", h=2)[:, :, 0:O, :],
                in_=w4_raw[e][:].rearrange("p t (h c) -> p h c t", h=2),
            )

        def quantise_w4(e):
            w4_codes = w_mx.tile([P, 4 * O], U32, align_bytes=64)
            w4_scales = w_mx.tile([P, 4 * O], U8, align_bytes=64)
            nc.vector.quantize_mx(
                out=w4_codes[:].bitcast(FP8X4),
                scales=w4_scales[:],
                in_=w4_grouped[:, e].rearrange("p c t -> p (c t)"),
            )
            w4_mx[e] = (w4_codes, w4_scales)

        groups = [(i, PAIR) for i in range(0, N_CHUNKS - SINGLES, PAIR)] + [
            (i, 1) for i in range(N_CHUNKS - SINGLES, N_CHUNKS)
        ]
        group_of = {i: g for g, (first, size) in enumerate(groups) for i in range(first, first + size)}
        h2_t = {}
        h2_grouped = {}
        h2_mx = {}
        h3_ps = {}
        h3_planes = {}
        h3_grouped = {}
        h3_mx = {}
        mean_ps = {}
        raw_ps = {}
        mean_sb = {}
        tanh_sb = {}
        logvar_sb = {}

        def transpose_h2(i, banks=(0, 1)):
            words = h2_raw[i][:].bitcast(F32)
            for b in banks:
                xt = psum_t.tile([P, 2, 2, P], F32)
                for j in range(2):
                    for u in range(2):
                        first = (2 * b + j) * (H // 2) + u * P
                        nc.tensor.transpose(xt[:, j, u, :], words[:, first : first + P], identity[:])
                h2_t[i, b] = xt
            if 1 in banks and live(i + H2_BUFS):
                load_chunk(i + H2_BUFS)

        def copy_h2(i, banks=(0, 1)):
            if 0 in banks:
                grouped = stage.tile([P, CHUNK * PACK], BF16, align_bytes=64, tag="h2_grouped")
                h2_grouped[i] = grouped
            grouped_words = h2_grouped[i][:].bitcast(F32)
            for b in banks:
                on_vector = b == 1 and (i == 1 or VECTOR_COPIES(i))
                (nc.vector.tensor_copy if on_vector else nc.scalar.copy)(
                    out=grouped_words[:, b * CHUNK : (b + 1) * CHUNK].rearrange(
                        "p (j c u) -> p j c u", j=2, u=2
                    ),
                    in_=h2_t[i, b][:].rearrange("p j u c -> p j c u"),
                )

        WHOLE = slice(0, CHUNK)
        HALVES = (slice(0, CHUNK // 2), slice(CHUNK // 2, CHUNK))

        def quantise_h2(i, cols=WHOLE):
            if cols.start == 0:
                codes = stage.tile([P, CHUNK], U32, align_bytes=64, tag="h2_codes")
                scales = stage.tile([P, CHUNK], U8, align_bytes=64, tag="h2_scales")
                h2_mx[i] = (codes, scales)
            codes, scales = h2_mx[i]
            nc.vector.quantize_mx(
                out=codes[:, cols].bitcast(FP8X4),
                scales=scales[:, cols],
                in_=h2_grouped[i][:, cols.start * PACK : cols.stop * PACK],
            )

        def first_product(i, planes=range(PACK), cols=WHOLE):
            w3_codes, w3_scales = w3_mx[i // CHUNKS_PER_MEMBER]
            h2_codes, h2_scales = h2_mx[i]
            for t in planes:
                features = slice(t * P, (t + 1) * P)
                if cols.start == 0:
                    acc = psum_1.tile([P, CHUNK], F32)
                    h3_ps[i, t] = acc
                nc.tensor.matmul_mx(
                    out=h3_ps[i, t][:, cols],
                    lhsT=w3_codes[:, features].bitcast(FP8X4),
                    lhsT_scale=w3_scales[:, features],
                    rhs=h2_codes[:, cols].bitcast(FP8X4),
                    rhs_scale=h2_scales[:, cols],
                    start=True,
                    stop=True,
                )

        def silu_h3(i, planes_now=range(PACK), cols=WHOLE):
            e = i // CHUNKS_PER_MEMBER
            group = group_of[i]
            first, size = groups[group]
            if group not in h3_planes:
                planes = h3_in.tile([P, PACK, size * CHUNK], BF16, tag="planes")
                h3_planes[group] = planes
            at = (i - first) * CHUNK
            for t in planes_now:
                nc.scalar.activation(
                    out=h3_planes[group][:, t, at + cols.start : at + cols.stop],
                    in_=h3_ps[i, t][:, cols],
                    func=ACT.Silu,
                    bias=b3_cols[:, e * PACK + t : e * PACK + t + 1],
                )

        def regroup_h3(group):
            size = groups[group][1]
            grouped = h3_stage.tile([P, size * CHUNK, PACK], BF16, align_bytes=64, tag="grouped")
            regroup(grouped[:], h3_planes[group][:])
            h3_grouped[group] = grouped

        def quantise_h3(group):
            size = groups[group][1]
            codes = h3_stage.tile([P, size * CHUNK], U32, align_bytes=64, tag="codes")
            scales = h3_stage.tile([P, size * CHUNK], U8, align_bytes=64, tag="scales")
            nc.vector.quantize_mx(
                out=codes[:].bitcast(FP8X4),
                scales=scales[:],
                in_=h3_grouped[group][:].rearrange("p c t -> p (c t)"),
            )
            h3_mx[group] = (codes, scales)

        def second_product(group):
            first, size = groups[group]
            w4_codes, w4_scales = w4_mx[first // CHUNKS_PER_MEMBER]
            h3_codes, h3_scales = h3_mx[group]
            pair = first // PAIR
            if first % PAIR == 0:
                if pair != N_PAIRS - 2:
                    raw_acc = psum_raw.tile([P, CHUNK], F32)
                    mean_acc = psum_mean.tile([P, PAIR_ROWS, O], F32)
                else:
                    raw_acc = psum_t.tile([P, CHUNK], F32, tag="xt")
                    mean_acc = psum_t.tile([P, PAIR_ROWS, O], F32, tag="xt")
                raw_ps[pair] = raw_acc
                mean_ps[pair] = mean_acc
            for j in range(size):
                half = (first + j) % PAIR
                cols = slice(j * CHUNK, (j + 1) * CHUNK)
                nc.tensor.matmul_mx(
                    out=raw_ps[pair][:],
                    lhsT=w4_codes[:, RAW_HALF[half]].bitcast(FP8X4),
                    lhsT_scale=w4_scales[:, RAW_HALF[half]],
                    rhs=h3_codes[:, cols].bitcast(FP8X4),
                    rhs_scale=h3_scales[:, cols],
                    start=(half == 0),
                    stop=(half == PAIR - 1),
                )
            for r in range(size * TILES):
                rows = slice(r * P, (r + 1) * P)
                nc.tensor.matmul_mx(
                    out=mean_ps[pair][:, first % PAIR * TILES + r, :],
                    lhsT=h3_codes[:, rows].bitcast(FP8X4),
                    lhsT_scale=h3_scales[:, rows],
                    rhs=w4_codes[:, MEAN_COLS].bitcast(FP8X4),
                    rhs_scale=w4_scales[:, MEAN_COLS],
                    start=True,
                    stop=True,
                )

        def tanh_raw(pair):
            e = pair * PAIR // CHUNKS_PER_MEMBER
            th = tanhs.tile([P, CHUNK], F32)
            nc.scalar.activation(
                out=th[:], in_=raw_ps[pair][:], func=ACT.Tanh, bias=tanh_bias[:, e : e + 1], scale=0.5
            )
            tanh_sb[pair] = th

        def shift_mean(pair):
            e, h = divmod(pair, CHUNKS_PER_MEMBER // PAIR)
            if h == 0:
                mean_member = outs.tile([P, ROWS_PER_PARTITION, O], F32)
                mean_sb[e] = mean_member
            rows = slice(h * PAIR_ROWS, (h + 1) * PAIR_ROWS)
            nc.vector.tensor_tensor(
                out=mean_sb[e][:, rows, :],
                in0=mean_ps[pair][:],
                in1=mean_shift[:, e, :].unsqueeze(1).to_broadcast([P, PAIR_ROWS, O]),
                op=ALU.add,
            )
            nc.sync.dma_start(out=mean_rows[e][:, rows, :], in_=mean_sb[e][:, rows, :])

        def logarithm(pair):
            nc.scalar.activation(
                out=tanh_sb[pair][:],
                in_=tanh_sb[pair][:],
                func=ACT.Ln,
                bias=middle[:],
                scale=half_span[:],
            )

        def stretch(pair):
            nc.vector.tensor_scalar(
                out=tanh_sb[pair][:],
                in0=tanh_sb[pair][:],
                scalar1=half_span[:],
                scalar2=middle[:],
                op0=ALU.mult,
                op1=ALU.add,
            )

        def finish(pair, leave):
            acc = psum_1.tile([P, TILES, PAIR, O], F32)
            for r in range(TILES):
                nc.tensor.transpose(
                    acc[:, r, :, :].rearrange("p a o -> p (a o)"),
                    tanh_sb[pair][:, r * P : (r + 1) * P],
                    identity[:],
                )
            e, h = divmod(pair, CHUNKS_PER_MEMBER // PAIR)
            logvar_pair = tanh_sb[pair][:].rearrange("p (a r o) -> p a r o", a=PAIR, r=TILES)
            for a in (slice(0, PAIR),) if pair < N_PAIRS - 1 else (slice(0, 1), slice(1, 2)):
                leave(out=logvar_pair[:, a].rearrange("p a r o -> p r a o"), in_=acc[:, :, a, :])
                rows = slice(h * PAIR_ROWS + a.start * TILES, h * PAIR_ROWS + a.stop * TILES)
                nc.sync.dma_start(
                    out=logvar_rows[e][:, rows, :],
                    in_=logvar_pair[:, a].rearrange("p a r o -> p (a r) o"),
                )

        def first_chunk_of_member(i):
            return live(i) and i % CHUNKS_PER_MEMBER == 0

        with tc.manual_schedule():
            parts = w3_parts(PACK)
            new_w3(0)
            for cols in parts[:2]:
                regroup_w3(0, cols)
            for cols in parts[:2]:
                quantise_w3(0, cols)
            keep_tensor_busy(HEAD_IDLE)
            transpose_h2(0)
            copy_h2(0)
            cast_b3()
            b3_ps = transpose_b3()
            nc.scalar.copy(out=b3_cols[:], in_=b3_ps[:])
            for cols in HALVES:
                quantise_h2(0, cols)
                first_product(0, range(2), cols)
                silu_h3(0, range(2), cols)
            for cols in parts[2:]:
                regroup_w3(0, cols)
            for cols in parts[2:]:
                quantise_w3(0, cols)
            transpose_h2(1)
            first_product(0, range(2, PACK))
            copy_h2(1)
            quantise_h2(1)
            silu_h3(0, range(2, PACK))
            transpose_h2(2)
            first_product(1)
            cast_bounds()
            regroup_w4(0)
            quantise_w4(0)

            def take_ln(out, in_):
                nc.scalar.activation(out=out, in_=in_, func=ACT.Ln, bias=zero[:])

            W = {}
            for e in range(1, E):
                a, b, c, d = WSTEP
                W.setdefault(max(4 * e - 2 - a, 0), []).append((new_w3, e))
                for lead, f in ((a, lambda e: regroup_w3(e, w3_parts(2)[0])), (b, lambda e: regroup_w3(e, w3_parts(2)[1])), (c, quantise_w3)):
                    W.setdefault(max(4 * e - 2 - lead, 0), []).append((f, e))
                W.setdefault(max(4 * e + 2 - d, 0), []).append((lambda e: (regroup_w4(e), quantise_w4(e)), e))
            RS, QS, MS, TS = {}, {}, {}, {}
            for g, (first, size) in enumerate(groups):
                last = first + size - 1
                r = last - 1 + LAG if size == 2 else last
                q = r + 1 if size == 2 and last < N_CHUNKS - 1 - SINGLES else r
                RS.setdefault(r, []).append(g)
                QS.setdefault(q, []).append(g)
                if last % 2 == 1:
                    if last // 2 < N_PAIRS - LATE_MEANS:
                        MS.setdefault(q + 1 if last // 2 < N_PAIRS - 3 else M7, []).append(last // 2)
                    TS.setdefault(q + 1, []).append(last // 2)
            for s in range(N_CHUNKS + 8):
                if live(s + LOOK):
                    copy_h2(s + LOOK)
                ending = s >= N_CHUNKS - 3
                if not ending:
                    for p in TS.pop(s, ()):
                        tanh_raw(p)
                if live(s + 1):
                    silu_h3(s + 1)
                for p in TS.pop(s, ()):
                    tanh_raw(p)
                if MFIRST or s == N_CHUNKS - 1:
                    for p in MS.pop(s, ()):
                        shift_mean(p)
                for g in RS.get(s, ()):
                    regroup_h3(g)
                    if groups[g][1] == 2 and live(s + LOOK):
                        pass
                for g in QS.get(s, ()):
                    if groups[g][1] == 2 and g not in RS.get(s, ()):
                        quantise_h3(g)
                if live(s + LOOK):
                    quantise_h2(s + LOOK)
                for g in QS.get(s, ()):
                    if groups[g][1] == 2 and g in RS.get(s, ()):
                        quantise_h3(g)
                for p in MS.pop(s, ()):
                    shift_mean(p)
                for g in QS.get(s, ()):
                    if groups[g][1] == 1:
                        quantise_h3(g)
                if s == 0:
                    bound_ps = transpose_bounds()
                    spread_vectors()
                    nc.scalar.copy(out=bound_cols[:], in_=bound_ps[:])
                    prepare_tanh_bias()
                if s == 1:
                    prepare_exps()
                if s == 3:
                    finish_exps()
                for f, e in W.pop(s, ()):
                    f(e)
                if live(s + LOOK + 1):
                    transpose_h2(s + LOOK + 1)
                if s % 2 == 1 and 1 < s < 16:
                    keep_tensor_busy(STEP_IDLE)
                if live(s + 2) and ending:
                    first_product(s + 2)
                for g in QS.get(s, ()):
                    second_product(g)
                if live(s + 2) and not ending:
                    first_product(s + 2)
            zero = const.tile([P, 1], F32)
            nc.scalar.activation(
                out=zero[:], in_=tanh_sb[N_PAIRS - 1][:, 0:1], func=ACT.Ln, bias=1.0, scale=0.0
            )
            for p in range(N_PAIRS - LATE_MEANS, N_PAIRS - 1):
                shift_mean(p)
            for q in range(N_PAIRS):
                stretch(q)
                if q == 3:
                    shift_mean(N_PAIRS - 1)
            for q in range(N_PAIRS):
                finish(q, take_ln)
